import numpy as np
import ml_dtypes


def mxq(x, axis, fmt="e4m3"):
    dtype, down = {"e4m3": (ml_dtypes.float8_e4m3fn, 7), "e5m2": (ml_dtypes.float8_e5m2, 14)}[fmt]
    v = np.moveaxis(np.asarray(x, np.float32).astype(ml_dtypes.bfloat16).astype(np.float64), axis, -1)
    blocks = v.reshape(v.shape[:-1] + (-1, 32))
    amax = np.abs(blocks).max(-1, keepdims=True)
    byte = np.maximum(np.where(amax > 0, np.frexp(amax)[1] - 1 + 127, 0) - down, 1)
    scale = np.exp2(byte - 127.0)
    codes = (blocks / scale).astype(np.float32).astype(dtype).astype(np.float64)
    return np.moveaxis((codes * scale).reshape(v.shape), -1, axis)


WIDE = False


def mx_kscale(k):
    if not WIDE:
        return np.ones(k)
    levels = np.array([10, -10, 5, -5, 0])
    if k % 512:
        return np.exp2(np.random.permutation(np.resize(levels, k // 32))).repeat(32)
    a = np.empty((k // 512, 16))
    for p in range(k // 512):
        a[p, :8] = np.random.permutation(np.resize(levels, 8))
        for g in range(8):
            far = levels[np.abs(levels - a[p, g]) >= 10]
            a[p, g + 8] = far[np.random.randint(len(far))]
    return np.exp2(a.ravel()).repeat(32)


BF16 = ml_dtypes.bfloat16


def bf(x):
    return np.asarray(x, np.float32).astype(BF16)


def f64(x):
    return np.asarray(x).astype(np.float64)


B, S, DM, H, DH, QB = 1, 1024, 1024, 8, 256, 512
DI = H * DH
EPS_GN = 1e-5


def setup_inputs():
    s = mx_kscale(DI)
    h = np.random.standard_normal((B, S, H, DH)) * 0.15 + np.random.standard_normal((B, 1, H, 1)) * 0.15
    return {"h_attn": bf(h.reshape(B, S, DI)),
            "gn_w": bf((1.0 + 0.1 * np.random.standard_normal(DI)) * s),
            "gn_b": bf(0.1 * np.random.standard_normal(DI) * s),
            "W_out": bf(np.random.standard_normal((DM, DI)) / np.sqrt(DI) / s[None, :]),
            "x": bf(np.random.standard_normal((B, S, DM))),
            "skip_scale": bf(0.7 + 0.1 * np.random.standard_normal(1))}


def reference(h_attn, gn_w, gn_b, W_out, x, skip_scale):
    hg = f64(h_attn).reshape(B, S, H, DH)
    mu = hg.mean(axis=(1, 3), keepdims=True)
    var = hg.var(axis=(1, 3), keepdims=True)
    hg = (hg - mu) / np.sqrt(var + EPS_GN)
    h = hg.reshape(B, S, DI) * f64(gn_w) + f64(gn_b)
    return (mxq(h, 2, "e4m3") @ mxq(f64(W_out), 1, "e4m3").T) + f64(skip_scale) * f64(x)

@@ -1,0 +1,287 @@
+from contextlib import ExitStack
+
+import concourse.mybir as mybir
+from concourse.masks import make_identity
+
+F32 = mybir.dt.float32
+BF16 = mybir.dt.bfloat16
+U32 = mybir.dt.uint32
+U8 = mybir.dt.uint8
+FP8X4 = mybir.dt.float8_e4m3fn_x4
+ALU = mybir.AluOpType
+ACT = mybir.ActivationFunctionType
+
+P = 128
+PACK = 4
+K_PASS = P * PACK
+S = 1024
+DI = 2048
+DM = 1024
+GROUP = 256
+EPS_GN = 1e-5
+PASSES = DI // K_PASS
+GROUPS_PER_PASS = K_PASS // GROUP
+ROW_TILES = S // P
+W_TILES = DM // P
+N_TILE = 512
+N_HALVES = DM // N_TILE
+PSUM_BANKS = 8
+FIRST_SHARED_PASS = 2
+UNIT_TILES = 4
+UNIT_ROWS = UNIT_TILES * P
+UNITS_PER_PASS = ROW_TILES // UNIT_TILES
+UNITS = PASSES * UNITS_PER_PASS
+FIRST_W_UNIT = 3
+OPEN_TILES = PSUM_BANKS - 1
+
+FLOPS = 2 * S * DM * DI
+
+
+def tile_mlstmblock_pb_kernel(tc, h_attn, gn_w, gn_b, W_out, x, skip_scale, out):
+    nc = tc.nc
+    h_rows = h_attn.flatten_outer_dims().rearrange("(p j) c -> p j c", j=ROW_TILES)
+    x_rows = x.flatten_outer_dims().rearrange("(p j) m -> p j m", j=ROW_TILES)
+    out_rows = out.flatten_outer_dims().rearrange("(p j) m -> p j m", j=ROW_TILES)
+    w_rows = W_out.rearrange("(t p) c -> p t c", p=P)
+
+    with ExitStack() as ctx:
+        ctx.enter_context(tc.manual_schedule())
+        keep = ctx.enter_context(tc.tile_pool(name="keep", bufs=1))
+        small = ctx.enter_context(tc.tile_pool(name="small", bufs=2))
+        stage = ctx.enter_context(tc.tile_pool(name="stage", bufs=2))
+        results = ctx.enter_context(tc.tile_pool(name="results", bufs=4))
+        stats_bank = ctx.enter_context(tc.psum_pool(name="stats_bank", bufs=1))
+        psum = ctx.enter_context(tc.psum_pool(name="psum", bufs=PSUM_BANKS - 1))
+
+        gn_w_sb = keep.tile([P, PASSES, PACK], BF16)
+        nc.sync.dma_start(out=gn_w_sb[:], in_=gn_w.rearrange("(g p t) -> p g t", p=P, t=PACK))
+        gn_b_sb = keep.tile([P, PASSES, PACK], BF16)
+        nc.sync.dma_start(out=gn_b_sb[:], in_=gn_b.rearrange("(g p t) -> p g t", p=P, t=PACK))
+        h_raw = [keep.tile([P, ROW_TILES, K_PASS], BF16, name="h_raw%d" % g) for g in range(PASSES)]
+        w_raw = [keep.tile([P, W_TILES, K_PASS], BF16, name="w_raw%d" % g) for g in range(PASSES)]
+        for g in range(PASSES):
+            nc.sync.dma_start(out=h_raw[g][:], in_=h_rows[:, :, g * K_PASS : (g + 1) * K_PASS])
+        for g in range(PASSES):
+            nc.sync.dma_start(out=w_raw[g][:], in_=w_rows[:, :, g * K_PASS : (g + 1) * K_PASS])
+        x_sb = keep.tile([P, ROW_TILES, DM], BF16)
+        nc.sync.dma_start(out=x_sb[:], in_=x_rows)
+        skip_bf = keep.tile([P, 1], BF16)
+        nc.sync.dma_start(out=skip_bf[:], in_=skip_scale.partition_broadcast(P))
+
+        ident_f32 = keep.tile([P, P], F32)
+        make_identity(nc, ident_f32[:])
+        ident_bf = keep.tile([P, P], BF16)
+        make_identity(nc, ident_bf[:])
+        mean_of = []
+        minus_mean_of = []
+        half = P // GROUPS_PER_PASS
+        for u in range(GROUPS_PER_PASS):
+            for sign, matrices in ((1.0, mean_of), (-1.0, minus_mean_of)):
+                matrix = keep.tile([P, P], F32, name="mean_matrix%d_%d" % (u, int(sign) + 1))
+                nc.vector.memset(matrix[:], 0.0)
+                nc.vector.memset(matrix[:, u * half : (u + 1) * half], sign / (S * GROUP))
+                matrices.append(matrix)
+        minus_half = keep.tile([P, 1], F32)
+        nc.vector.memset(minus_half[:], -0.5)
+
+        h_codes = keep.tile([P, PASSES, S], U32, align_bytes=64)
+        h_scales = keep.tile([P, PASSES, S], U8, align_bytes=64)
+        w_codes = keep.tile([P, PASSES, DM], U32, align_bytes=64)
+        w_scales = keep.tile([P, PASSES, DM], U8, align_bytes=64)
+        stats_ps = stats_bank.tile([P, PASSES, 2], F32)
+        sum_part = [keep.tile([P, GROUPS_PER_PASS], F32, name="sum_part%d" % g) for g in range(PASSES)]
+        sumsq_part = [
+            [keep.tile([P, 1], F32, name="sumsq_part%d_%d" % (g, u)) for u in range(GROUPS_PER_PASS)]
+            for g in range(PASSES)
+        ]
+        quad = [P, PACK]
+        gain = [keep.tile(quad, F32, name="gain%d" % g) for g in range(PASSES)]
+        shift = [keep.tile(quad, F32, name="shift%d" % g) for g in range(PASSES)]
+
+        def sums(g):
+            for u in range(GROUPS_PER_PASS):
+                scratch = stage.tile([P, ROW_TILES, GROUP], BF16, name="scratch_v")
+                nc.vector.tensor_scalar(
+                    out=scratch[:],
+                    in0=h_raw[g][:, :, u * GROUP : (u + 1) * GROUP],
+                    scalar1=1.0,
+                    scalar2=None,
+                    op0=ALU.mult,
+                    op1=ALU.add,
+                    accum_out=sum_part[g][:, u : u + 1],
+                )
+
+        def squares_on_scalar(g, u):
+            scratch = stage.tile([P, ROW_TILES, GROUP], BF16, name="scratch_s")
+            nc.scalar.activation(
+                out=scratch[:],
+                in_=h_raw[g][:, :, u * GROUP : (u + 1) * GROUP],
+                func=ACT.Square,
+                accum_out=sumsq_part[g][u][:],
+            )
+
+        def squares_on_vector(g, u):
+            group = h_raw[g][:, :, u * GROUP : (u + 1) * GROUP]
+            scratch = stage.tile([P, ROW_TILES, GROUP], BF16, name="scratch_v")
+            nc.vector.scalar_tensor_tensor(
+                out=scratch[:], in0=group, scalar=1.0, in1=group, op0=ALU.mult, op1=ALU.mult,
+                accum_out=sumsq_part[g][u][:],
+            )
+
+        def totals(g):
+            for u in range(GROUPS_PER_PASS):
+                ends = {"start": u == 0, "stop": u == GROUPS_PER_PASS - 1}
+                nc.tensor.matmul(out=stats_ps[:, g, 0:1], lhsT=minus_mean_of[u][:], rhs=sum_part[g][:, u : u + 1], **ends)
+            for u in range(GROUPS_PER_PASS):
+                ends = {"start": u == 0, "stop": u == GROUPS_PER_PASS - 1}
+                nc.tensor.matmul(out=stats_ps[:, g, 1:2], lhsT=mean_of[u][:], rhs=sumsq_part[g][u][:], **ends)
+
+        def gain_and_shift(g):
+            moments = small.tile([P, 2], F32, name="moments")
+            nc.vector.tensor_copy(out=moments[:], in_=stats_ps[:, g, :])
+            minus_mean = moments[:, 0:1]
+            var = small.tile([P, 1], F32, name="var")
+            rstd = small.tile([P, 1], F32, name="rstd")
+            nc.gpsimd.tensor_tensor(out=var[:], in0=minus_mean, in1=minus_mean, op=ALU.mult)
+            nc.gpsimd.tensor_tensor(out=var[:], in0=moments[:, 1:2], in1=var[:], op=ALU.subtract)
+            nc.gpsimd.tensor_scalar(out=var[:], in0=var[:], scalar1=1.0, scalar2=EPS_GN, op0=ALU.mult, op1=ALU.add)
+            nc.gpsimd.tensor_tensor(out=rstd[:], in0=var[:], in1=minus_half[:], op=ALU.pow)
+            nc.gpsimd.tensor_tensor(out=gain[g][:], in0=gn_w_sb[:, g, :], in1=rstd[:].to_broadcast(quad), op=ALU.mult)
+            nc.gpsimd.tensor_tensor(out=shift[g][:], in0=gain[g][:], in1=minus_mean.to_broadcast(quad), op=ALU.mult)
+            nc.gpsimd.tensor_tensor(out=shift[g][:], in0=shift[g][:], in1=gn_b_sb[:, g, :], op=ALU.add)
+
+        def transpose_activations(g, r):
+            quads = h_raw[g][:].rearrange("p j (q t) -> p j q t", t=PACK)
+            banks = []
+            for t in range(PACK):
+                hT_ps = psum.tile([P, UNIT_TILES, P], BF16, tag="bank", name="hT_ps")
+                for i in range(UNIT_TILES):
+                    nc.tensor.transpose(out=hT_ps[:, i, :], in_=quads[:, r * UNIT_TILES + i, :, t], identity=ident_bf[:])
+                banks.append(hT_ps)
+            return banks
+
+        def normalise(g, banks, planes, t, on_scalar):
+            bank = banks[t][:].rearrange("p i r -> p (i r)")
+            if on_scalar:
+                nc.scalar.activation(
+                    out=planes[:, t, :], in_=bank, func=ACT.Identity,
+                    scale=gain[g][:, t : t + 1], bias=shift[g][:, t : t + 1],
+                )
+            else:
+                nc.vector.tensor_scalar(
+                    out=planes[:, t, :], in0=bank, scalar1=gain[g][:, t : t + 1],
+                    scalar2=shift[g][:, t : t + 1], op0=ALU.mult, op1=ALU.add,
+                )
+
+        def vector_planes(g):
+            return PACK if g < FIRST_SHARED_PASS else PACK // 2
+
+        def regroup(planes):
+            grouped = stage.tile([P, UNIT_ROWS, PACK], BF16, align_bytes=64, name="h_grouped")
+            nc.vector.tensor_copy(
+                out=grouped[:].rearrange("p (c i) t -> p c t i", i=4),
+                in_=planes[:].rearrange("p t (c i) -> p c t i", i=4),
+            )
+            return grouped
+
+        def quantise_activations(g, r, grouped):
+            rows = slice(r * UNIT_ROWS, (r + 1) * UNIT_ROWS)
+            nc.vector.quantize_mx(
+                out=h_codes[:, g, rows].bitcast(FP8X4),
+                scales=h_scales[:, g, rows],
+                in_=grouped[:].rearrange("p s t -> p (s t)"),
+            )
+
+        def transpose_weights(g):
+            grouped = keep.tile([P, DM * PACK], BF16, align_bytes=64, name="w_grouped%d" % g)
+            grouped_words = grouped[:].bitcast(F32).rearrange("p (a c m u) -> p a c m u", a=W_TILES // 2, c=2, u=2)
+            for a in range(W_TILES // 2):
+                wT_ps = psum.tile([P, 2, 2, P], F32, tag="bank", name="wT_ps")
+                for c in range(2):
+                    words = w_raw[g][:, 2 * a + c, :].bitcast(F32).rearrange("p (q u) -> p u q", u=2)
+                    for u in range(2):
+                        nc.tensor.transpose(out=wT_ps[:, c, u, :], in_=words[:, u, :], identity=ident_f32[:])
+                nc.scalar.copy(out=grouped_words[:, a], in_=wT_ps[:].rearrange("p c u m -> p c m u"))
+            return grouped
+
+        def quantise_weights(g, grouped):
+            nc.vector.quantize_mx(out=w_codes[:, g, :].bitcast(FP8X4), scales=w_scales[:, g, :], in_=grouped[:])
+
+        def multiply(acc, tile_index, g):
+            j, n = tile_index // N_HALVES, tile_index % N_HALVES
+            rows = slice(j * P, (j + 1) * P)
+            cols = slice(n * N_TILE, (n + 1) * N_TILE)
+            nc.tensor.matmul_mx(
+                out=acc[:],
+                lhsT=h_codes[:, g, rows].bitcast(FP8X4),
+                lhsT_scale=h_scales[:, g, rows],
+                rhs=w_codes[:, g, cols].bitcast(FP8X4),
+                rhs_scale=w_scales[:, g, cols],
+                start=(g == 0),
+                stop=(g == PASSES - 1),
+            )
+
+        def finish(acc, tile_index):
+            j, n = tile_index // N_HALVES, tile_index % N_HALVES
+            cols = slice(n * N_TILE, (n + 1) * N_TILE)
+            result = results.tile([P, N_TILE], F32, name="result")
+            nc.vector.scalar_tensor_tensor(
+                out=result[:], in0=x_sb[:, j, cols], scalar=skip[:, 0:1], in1=acc[:], op0=ALU.mult, op1=ALU.add
+            )
+            nc.sync.dma_start(out=out_rows[:, j, cols], in_=result[:])
+
+        banks = transpose_activations(0, 0)
+        sums(0)
+        squares_on_scalar(0, 0)
+        squares_on_vector(0, 1)
+        totals(0)
+        gain_and_shift(0)
+        sums(1)
+        squares_on_scalar(1, 0)
+        squares_on_scalar(1, 1)
+        totals(1)
+        planes = stage.tile([P, PACK, UNIT_ROWS], BF16, name="planes")
+
+        w_grouped = {}
+        for k in range(UNITS):
+            g, r = k // UNITS_PER_PASS, k % UNITS_PER_PASS
+            new_pass = r == 0
+            if new_pass and g + 2 < PASSES:
+                squares_on_scalar(g + 2, 0)
+                squares_on_scalar(g + 2, 1)
+            if new_pass and g + 1 < PASSES:
+                gain_and_shift(g + 1)
+            for t in range(vector_planes(g)):
+                normalise(g, banks, planes, t, False)
+            if new_pass and g + 2 < PASSES:
+                sums(g + 2)
+            if k + 1 < UNITS:
+                next_g, next_r = (k + 1) // UNITS_PER_PASS, (k + 1) % UNITS_PER_PASS
+                next_banks = transpose_activations(next_g, next_r)
+                next_planes = stage.tile([P, PACK, UNIT_ROWS], BF16, name="planes")
+                for t in range(vector_planes(next_g), PACK):
+                    normalise(next_g, next_banks, next_planes, t, True)
+            if new_pass and g + 2 < PASSES:
+                totals(g + 2)
+            if 0 <= k - FIRST_W_UNIT < PASSES:
+                w_grouped[k - FIRST_W_UNIT] = transpose_weights(k - FIRST_W_UNIT)
+            grouped = regroup(planes)
+            if 0 <= k - FIRST_W_UNIT - 1 < PASSES:
+                quantise_weights(k - FIRST_W_UNIT - 1, w_grouped[k - FIRST_W_UNIT - 1])
+            quantise_activations(g, r, grouped)
+            if k + 1 < UNITS:
+                banks, planes = next_banks, next_planes
+        skip = keep.tile([P, 1], F32)
+        nc.vector.tensor_copy(out=skip[:], in_=skip_bf[:])
+
+        open_accs = [psum.tile([P, N_TILE], F32, tag="bank", name="acc") for i in range(OPEN_TILES)]
+        for g in range(PASSES):
+            for i in range(OPEN_TILES):
+                multiply(open_accs[i], i, g)
+        for i in range(OPEN_TILES):
+            finish(open_accs[i], i)
+        for i in range(OPEN_TILES, ROW_TILES * N_HALVES):
+            acc = psum.tile([P, N_TILE], F32, tag="bank", name="acc")
+            for g in range(PASSES):
+                multiply(acc, i, g)
+            finish(acc, i)

@@ -25,14 +25,17 @@ ROW_TILES = S // P
 W_TILES = DM // P
 N_TILE = 512
 N_HALVES = DM // N_TILE
-PSUM_BANKS = 8
-FIRST_SHARED_PASS = 2
 UNIT_TILES = 4
 UNIT_ROWS = UNIT_TILES * P
-UNITS_PER_PASS = ROW_TILES // UNIT_TILES
-UNITS = PASSES * UNITS_PER_PASS
-FIRST_W_UNIT = 3
-OPEN_TILES = PSUM_BANKS - 1
+HALVES = ROW_TILES // UNIT_TILES
+OPEN_TILES = 3
+OPEN1 = 3
+S_PLANES0 = 3
+S_PLANES1 = 4
+W_S = 4
+EPIS = 2
+MXS = 2
+LOADS = "h0 h1 w0 h2 w1 h3 w2 w3"
 
 FLOPS = 2 * S * DM * DI
 
@@ -48,39 +51,42 @@ def tile_mlstmblock_pb_kernel(tc, h_attn, gn_w, gn_b, W_out, x, skip_scale, out)
         ctx.enter_context(tc.manual_schedule())
         keep = ctx.enter_context(tc.tile_pool(name="keep", bufs=1))
         small = ctx.enter_context(tc.tile_pool(name="small", bufs=2))
-        stage = ctx.enter_context(tc.tile_pool(name="stage", bufs=2))
+        stage = ctx.enter_context(tc.tile_pool(name="stage", bufs=3))
         results = ctx.enter_context(tc.tile_pool(name="results", bufs=4))
         stats_bank = ctx.enter_context(tc.psum_pool(name="stats_bank", bufs=1))
-        psum = ctx.enter_context(tc.psum_pool(name="psum", bufs=PSUM_BANKS - 1))
+        turned = ctx.enter_context(tc.psum_pool(name="turned", bufs=7))
 
         gn_w_sb = keep.tile([P, PASSES, PACK], BF16)
-        nc.sync.dma_start(out=gn_w_sb[:], in_=gn_w.rearrange("(g p t) -> p g t", p=P, t=PACK))
         gn_b_sb = keep.tile([P, PASSES, PACK], BF16)
-        nc.sync.dma_start(out=gn_b_sb[:], in_=gn_b.rearrange("(g p t) -> p g t", p=P, t=PACK))
         h_raw = [keep.tile([P, ROW_TILES, K_PASS], BF16, name="h_raw%d" % g) for g in range(PASSES)]
         w_raw = [keep.tile([P, W_TILES, K_PASS], BF16, name="w_raw%d" % g) for g in range(PASSES)]
-        for g in range(PASSES):
-            nc.sync.dma_start(out=h_raw[g][:], in_=h_rows[:, :, g * K_PASS : (g + 1) * K_PASS])
-        for g in range(PASSES):
-            nc.sync.dma_start(out=w_raw[g][:], in_=w_rows[:, :, g * K_PASS : (g + 1) * K_PASS])
         x_sb = keep.tile([P, ROW_TILES, DM], BF16)
-        nc.sync.dma_start(out=x_sb[:], in_=x_rows)
         skip_bf = keep.tile([P, 1], BF16)
+        first = True
+        for item in LOADS.split(" "):
+            g = int(item[1])
+            if item[0] == "h":
+                nc.sync.dma_start(out=h_raw[g][:], in_=h_rows[:, :, g * K_PASS : (g + 1) * K_PASS])
+            else:
+                nc.sync.dma_start(out=w_raw[g][:], in_=w_rows[:, :, g * K_PASS : (g + 1) * K_PASS])
+            if first:
+                nc.sync.dma_start(out=gn_w_sb[:], in_=gn_w.rearrange("(g p t) -> p g t", p=P, t=PACK))
+                nc.sync.dma_start(out=gn_b_sb[:], in_=gn_b.rearrange("(g p t) -> p g t", p=P, t=PACK))
+                first = False
+        nc.sync.dma_start(out=x_sb[:], in_=x_rows)
         nc.sync.dma_start(out=skip_bf[:], in_=skip_scale.partition_broadcast(P))
 
         ident_f32 = keep.tile([P, P], F32)
         make_identity(nc, ident_f32[:])
-        ident_bf = keep.tile([P, P], BF16)
-        make_identity(nc, ident_bf[:])
+        ones = keep.tile([P, 1], BF16)
+        nc.vector.memset(ones[:], 1.0)
         mean_of = []
-        minus_mean_of = []
         half = P // GROUPS_PER_PASS
         for u in range(GROUPS_PER_PASS):
-            for sign, matrices in ((1.0, mean_of), (-1.0, minus_mean_of)):
-                matrix = keep.tile([P, P], F32, name="mean_matrix%d_%d" % (u, int(sign) + 1))
-                nc.vector.memset(matrix[:], 0.0)
-                nc.vector.memset(matrix[:, u * half : (u + 1) * half], sign / (S * GROUP))
-                matrices.append(matrix)
+            matrix = keep.tile([P, P], F32, name="mean_matrix%d" % u)
+            nc.vector.memset(matrix[:], 0.0)
+            nc.vector.memset(matrix[:, u * half : (u + 1) * half], 1.0 / (S * GROUP))
+            mean_of.append(matrix)
         minus_half = keep.tile([P, 1], F32)
         nc.vector.memset(minus_half[:], -0.5)
 
@@ -88,36 +94,31 @@ def tile_mlstmblock_pb_kernel(tc, h_attn, gn_w, gn_b, W_out, x, skip_scale, out)
         h_scales = keep.tile([P, PASSES, S], U8, align_bytes=64)
         w_codes = keep.tile([P, PASSES, DM], U32, align_bytes=64)
         w_scales = keep.tile([P, PASSES, DM], U8, align_bytes=64)
-        stats_ps = stats_bank.tile([P, PASSES, 2], F32)
-        sum_part = [keep.tile([P, GROUPS_PER_PASS], F32, name="sum_part%d" % g) for g in range(PASSES)]
-        sumsq_part = [
-            [keep.tile([P, 1], F32, name="sumsq_part%d_%d" % (g, u)) for u in range(GROUPS_PER_PASS)]
-            for g in range(PASSES)
-        ]
+        stats_ps = stats_bank.tile([P, PASSES, 4], F32)
+        part = [keep.tile([P, GROUPS_PER_PASS, 2], F32, name="part%d" % g) for g in range(PASSES)]
         quad = [P, PACK]
         gain = [keep.tile(quad, F32, name="gain%d" % g) for g in range(PASSES)]
         shift = [keep.tile(quad, F32, name="shift%d" % g) for g in range(PASSES)]
+        skip = keep.tile([P, 1], F32)
 
         def sums(g):
             for u in range(GROUPS_PER_PASS):
-                scratch = stage.tile([P, ROW_TILES, GROUP], BF16, name="scratch_v")
-                nc.vector.tensor_scalar(
-                    out=scratch[:],
-                    in0=h_raw[g][:, :, u * GROUP : (u + 1) * GROUP],
-                    scalar1=1.0,
-                    scalar2=None,
-                    op0=ALU.mult,
-                    op1=ALU.add,
-                    accum_out=sum_part[g][:, u : u + 1],
-                )
+                for j in range(ROW_TILES):
+                    for c in range(2):
+                        at = u * GROUP + c * P
+                        nc.tensor.matmul(
+                            out=stats_ps[:, g, u : u + 1], lhsT=h_raw[g][:, j, at : at + P], rhs=ones[:],
+                            start=(j == 0 and c == 0), stop=(j == ROW_TILES - 1 and c == 1),
+                        )
+
+        def keep_sums(g):
+            nc.vector.tensor_copy(out=part[g][:, :, 0], in_=stats_ps[:, g, 0:2])
 
         def squares_on_scalar(g, u):
             scratch = stage.tile([P, ROW_TILES, GROUP], BF16, name="scratch_s")
             nc.scalar.activation(
-                out=scratch[:],
-                in_=h_raw[g][:, :, u * GROUP : (u + 1) * GROUP],
-                func=ACT.Square,
-                accum_out=sumsq_part[g][u][:],
+                out=scratch[:], in_=h_raw[g][:, :, u * GROUP : (u + 1) * GROUP], func=ACT.Square,
+                accum_out=part[g][:, u, 1:2],
             )
 
         def squares_on_vector(g, u):
@@ -125,56 +126,59 @@ def tile_mlstmblock_pb_kernel(tc, h_attn, gn_w, gn_b, W_out, x, skip_scale, out)
             scratch = stage.tile([P, ROW_TILES, GROUP], BF16, name="scratch_v")
             nc.vector.scalar_tensor_tensor(
                 out=scratch[:], in0=group, scalar=1.0, in1=group, op0=ALU.mult, op1=ALU.mult,
-                accum_out=sumsq_part[g][u][:],
+                accum_out=part[g][:, u, 1:2],
             )
 
         def totals(g):
             for u in range(GROUPS_PER_PASS):
-                ends = {"start": u == 0, "stop": u == GROUPS_PER_PASS - 1}
-                nc.tensor.matmul(out=stats_ps[:, g, 0:1], lhsT=minus_mean_of[u][:], rhs=sum_part[g][:, u : u + 1], **ends)
-            for u in range(GROUPS_PER_PASS):
-                ends = {"start": u == 0, "stop": u == GROUPS_PER_PASS - 1}
-                nc.tensor.matmul(out=stats_ps[:, g, 1:2], lhsT=mean_of[u][:], rhs=sumsq_part[g][u][:], **ends)
+                nc.tensor.matmul(
+                    out=stats_ps[:, g, 2:4], lhsT=mean_of[u][:], rhs=part[g][:, u, :],
+                    start=(u == 0), stop=(u == GROUPS_PER_PASS - 1),
+                )
 
         def gain_and_shift(g):
             moments = small.tile([P, 2], F32, name="moments")
-            nc.vector.tensor_copy(out=moments[:], in_=stats_ps[:, g, :])
-            minus_mean = moments[:, 0:1]
+            nc.vector.tensor_copy(out=moments[:], in_=stats_ps[:, g, 2:4])
+            mean = moments[:, 0:1]
             var = small.tile([P, 1], F32, name="var")
             rstd = small.tile([P, 1], F32, name="rstd")
-            nc.gpsimd.tensor_tensor(out=var[:], in0=minus_mean, in1=minus_mean, op=ALU.mult)
+            nc.gpsimd.tensor_tensor(out=var[:], in0=mean, in1=mean, op=ALU.mult)
             nc.gpsimd.tensor_tensor(out=var[:], in0=moments[:, 1:2], in1=var[:], op=ALU.subtract)
             nc.gpsimd.tensor_scalar(out=var[:], in0=var[:], scalar1=1.0, scalar2=EPS_GN, op0=ALU.mult, op1=ALU.add)
             nc.gpsimd.tensor_tensor(out=rstd[:], in0=var[:], in1=minus_half[:], op=ALU.pow)
             nc.gpsimd.tensor_tensor(out=gain[g][:], in0=gn_w_sb[:, g, :], in1=rstd[:].to_broadcast(quad), op=ALU.mult)
-            nc.gpsimd.tensor_tensor(out=shift[g][:], in0=gain[g][:], in1=minus_mean.to_broadcast(quad), op=ALU.mult)
-            nc.gpsimd.tensor_tensor(out=shift[g][:], in0=shift[g][:], in1=gn_b_sb[:, g, :], op=ALU.add)
+            nc.gpsimd.tensor_tensor(out=shift[g][:], in0=gain[g][:], in1=mean.to_broadcast(quad), op=ALU.mult)
+            nc.gpsimd.tensor_tensor(out=shift[g][:], in0=gn_b_sb[:, g, :], in1=shift[g][:], op=ALU.subtract)
 
-        def transpose_activations(g, r):
-            quads = h_raw[g][:].rearrange("p j (q t) -> p j q t", t=PACK)
+        def transpose_h(g, r):
+            words = h_raw[g][:].rearrange("p j c -> p (j c)").bitcast(F32).rearrange("p (j q u) -> p j u q", j=ROW_TILES, u=2)
             banks = []
-            for t in range(PACK):
-                hT_ps = psum.tile([P, UNIT_TILES, P], BF16, tag="bank", name="hT_ps")
+            for u in range(2):
+                bank = turned.tile([P, UNIT_TILES, P], F32, tag="bank", name="hT")
                 for i in range(UNIT_TILES):
-                    nc.tensor.transpose(out=hT_ps[:, i, :], in_=quads[:, r * UNIT_TILES + i, :, t], identity=ident_bf[:])
-                banks.append(hT_ps)
+                    nc.tensor.transpose(out=bank[:, i, :], in_=words[:, r * UNIT_TILES + i, u, :], identity=ident_f32[:])
+                banks.append(bank)
             return banks
 
         def normalise(g, banks, planes, t, on_scalar):
-            bank = banks[t][:].rearrange("p i r -> p (i r)")
+            u, e = t // 2, t % 2
+            values = banks[u][:].rearrange("p i r -> p (i r)").bitcast(BF16).rearrange("p (r e) -> p e r", e=2)[:, e, :]
             if on_scalar:
                 nc.scalar.activation(
-                    out=planes[:, t, :], in_=bank, func=ACT.Identity,
+                    out=planes[:, t, :], in_=values, func=ACT.Identity,
                     scale=gain[g][:, t : t + 1], bias=shift[g][:, t : t + 1],
                 )
             else:
                 nc.vector.tensor_scalar(
-                    out=planes[:, t, :], in0=bank, scalar1=gain[g][:, t : t + 1],
+                    out=planes[:, t, :], in0=values, scalar1=gain[g][:, t : t + 1],
                     scalar2=shift[g][:, t : t + 1], op0=ALU.mult, op1=ALU.add,
                 )
 
-        def vector_planes(g):
-            return PACK if g < FIRST_SHARED_PASS else PACK // 2
+        def normalise_all(g, banks, scalar_planes):
+            planes = stage.tile([P, PACK, UNIT_ROWS], BF16, name="planes")
+            for t in range(PACK):
+                normalise(g, banks, planes, t, t < scalar_planes)
+            return planes
 
         def regroup(planes):
             grouped = stage.tile([P, UNIT_ROWS, PACK], BF16, align_bytes=64, name="h_grouped")
@@ -184,45 +188,39 @@ def tile_mlstmblock_pb_kernel(tc, h_attn, gn_w, gn_b, W_out, x, skip_scale, out)
             )
             return grouped
 
-        def quantise_activations(g, r, grouped):
+        def quantise_h(g, r, grouped):
             rows = slice(r * UNIT_ROWS, (r + 1) * UNIT_ROWS)
             nc.vector.quantize_mx(
-                out=h_codes[:, g, rows].bitcast(FP8X4),
-                scales=h_scales[:, g, rows],
+                out=h_codes[:, g, rows].bitcast(FP8X4), scales=h_scales[:, g, rows],
                 in_=grouped[:].rearrange("p s t -> p (s t)"),
             )
 
-        def transpose_weights(g):
-            grouped = keep.tile([P, DM * PACK], BF16, align_bytes=64, name="w_grouped%d" % g)
+        def transpose_w(g, scalar_copies):
+            grouped = stage.tile([P, DM * PACK], BF16, align_bytes=64, name="w_grouped")
             grouped_words = grouped[:].bitcast(F32).rearrange("p (a c m u) -> p a c m u", a=W_TILES // 2, c=2, u=2)
             for a in range(W_TILES // 2):
-                wT_ps = psum.tile([P, 2, 2, P], F32, tag="bank", name="wT_ps")
+                bank = turned.tile([P, 2, 2, P], F32, tag="bank", name="wT")
                 for c in range(2):
                     words = w_raw[g][:, 2 * a + c, :].bitcast(F32).rearrange("p (q u) -> p u q", u=2)
                     for u in range(2):
-                        nc.tensor.transpose(out=wT_ps[:, c, u, :], in_=words[:, u, :], identity=ident_f32[:])
-                nc.scalar.copy(out=grouped_words[:, a], in_=wT_ps[:].rearrange("p c u m -> p c m u"))
+                        nc.tensor.transpose(out=bank[:, c, u, :], in_=words[:, u, :], identity=ident_f32[:])
+                copy = nc.scalar.copy if a < scalar_copies else nc.vector.tensor_copy
+                copy(out=grouped_words[:, a], in_=bank[:].rearrange("p c u m -> p c m u"))
             return grouped
 
-        def quantise_weights(g, grouped):
+        def quantise_w(g, grouped):
             nc.vector.quantize_mx(out=w_codes[:, g, :].bitcast(FP8X4), scales=w_scales[:, g, :], in_=grouped[:])
 
-        def multiply(acc, tile_index, g):
-            j, n = tile_index // N_HALVES, tile_index % N_HALVES
+        def multiply(acc, j, n, g):
             rows = slice(j * P, (j + 1) * P)
             cols = slice(n * N_TILE, (n + 1) * N_TILE)
             nc.tensor.matmul_mx(
-                out=acc[:],
-                lhsT=h_codes[:, g, rows].bitcast(FP8X4),
-                lhsT_scale=h_scales[:, g, rows],
-                rhs=w_codes[:, g, cols].bitcast(FP8X4),
-                rhs_scale=w_scales[:, g, cols],
-                start=(g == 0),
-                stop=(g == PASSES - 1),
+                out=acc[:], lhsT=h_codes[:, g, rows].bitcast(FP8X4), lhsT_scale=h_scales[:, g, rows],
+                rhs=w_codes[:, g, cols].bitcast(FP8X4), rhs_scale=w_scales[:, g, cols],
+                start=(g == 0), stop=(g == PASSES - 1),
             )
 
-        def finish(acc, tile_index):
-            j, n = tile_index // N_HALVES, tile_index % N_HALVES
+        def finish(acc, j, n):
             cols = slice(n * N_TILE, (n + 1) * N_TILE)
             result = results.tile([P, N_TILE], F32, name="result")
             nc.vector.scalar_tensor_tensor(
@@ -230,58 +228,78 @@ def tile_mlstmblock_pb_kernel(tc, h_attn, gn_w, gn_b, W_out, x, skip_scale, out)
             )
             nc.sync.dma_start(out=out_rows[:, j, cols], in_=result[:])
 
-        banks = transpose_activations(0, 0)
-        sums(0)
-        squares_on_scalar(0, 0)
-        squares_on_vector(0, 1)
-        totals(0)
-        gain_and_shift(0)
-        sums(1)
-        squares_on_scalar(1, 0)
-        squares_on_scalar(1, 1)
-        totals(1)
-        planes = stage.tile([P, PACK, UNIT_ROWS], BF16, name="planes")
+        def new_acc():
+            return turned.tile([P, N_TILE], F32, tag="bank", name="acc")
 
-        w_grouped = {}
-        for k in range(UNITS):
-            g, r = k // UNITS_PER_PASS, k % UNITS_PER_PASS
-            new_pass = r == 0
-            if new_pass and g + 2 < PASSES:
-                squares_on_scalar(g + 2, 0)
-                squares_on_scalar(g + 2, 1)
-            if new_pass and g + 1 < PASSES:
-                gain_and_shift(g + 1)
-            for t in range(vector_planes(g)):
-                normalise(g, banks, planes, t, False)
-            if new_pass and g + 2 < PASSES:
-                sums(g + 2)
-            if k + 1 < UNITS:
-                next_g, next_r = (k + 1) // UNITS_PER_PASS, (k + 1) % UNITS_PER_PASS
-                next_banks = transpose_activations(next_g, next_r)
-                next_planes = stage.tile([P, PACK, UNIT_ROWS], BF16, name="planes")
-                for t in range(vector_planes(next_g), PACK):
-                    normalise(next_g, next_banks, next_planes, t, True)
-            if new_pass and g + 2 < PASSES:
-                totals(g + 2)
-            if 0 <= k - FIRST_W_UNIT < PASSES:
-                w_grouped[k - FIRST_W_UNIT] = transpose_weights(k - FIRST_W_UNIT)
-            grouped = regroup(planes)
-            if 0 <= k - FIRST_W_UNIT - 1 < PASSES:
-                quantise_weights(k - FIRST_W_UNIT - 1, w_grouped[k - FIRST_W_UNIT - 1])
-            quantise_activations(g, r, grouped)
-            if k + 1 < UNITS:
-                banks, planes = next_banks, next_planes
-        skip = keep.tile([P, 1], F32)
-        nc.vector.tensor_copy(out=skip[:], in_=skip_bf[:])
-
-        open_accs = [psum.tile([P, N_TILE], F32, tag="bank", name="acc") for i in range(OPEN_TILES)]
-        for g in range(PASSES):
-            for i in range(OPEN_TILES):
-                multiply(open_accs[i], i, g)
-        for i in range(OPEN_TILES):
-            finish(open_accs[i], i)
-        for i in range(OPEN_TILES, ROW_TILES * N_HALVES):
-            acc = psum.tile([P, N_TILE], F32, tag="bank", name="acc")
+        tiles = [(j, n) for j in range(UNIT_TILES) for n in range(N_HALVES)]
+        tiles1 = [(j, n) for j in range(UNIT_TILES, ROW_TILES) for n in range(N_HALVES)]
+        open_accs = []
+        hb = {}
+        wg = {}
+        pl = {}
+        gr = {}
+        units = [(g, r) for r in range(HALVES) for g in range(PASSES)]
+        waiting = []
+        for k in range(len(units) + 2):
+            if k < PASSES:
+                squares_on_scalar(k, 0)
+            if 0 <= k - 2 < len(units):
+                g, r = units[k - 2]
+                gr[k - 2] = regroup(pl[k - 2])
+                if r == 0:
+                    quantise_w(g, wg[g])
+                else:
+                    for acc, (j, n) in waiting[:EPIS]:
+                        finish(acc, j, n)
+                    waiting = waiting[EPIS:]
+                quantise_h(g, r, gr[k - 2])
+            if k < PASSES:
+                squares_on_vector(k, 1)
+                sums(k)
+                keep_sums(k)
+            if k < len(units):
+                hb[k] = transpose_h(units[k][0], units[k][1])
+            if 0 <= k - 1 < len(units):
+                g, r = units[k - 1]
+                pl[k - 1] = normalise_all(g, hb[k - 1], S_PLANES0 if r == 0 else S_PLANES1)
+                if r == 0:
+                    wg[g] = transpose_w(g, W_S)
+            if k < PASSES:
+                totals(k)
+                gain_and_shift(k)
+            if 0 <= k - 2 < PASSES:
+                g = k - 2
+                if g == 0:
+                    open_accs = [new_acc() for i in range(OPEN_TILES)]
+                for i in range(OPEN_TILES):
+                    multiply(open_accs[i], tiles[i][0], tiles[i][1], g)
+                if g == PASSES - 1:
+                    nc.vector.tensor_copy(out=skip[:], in_=skip_bf[:])
+                    waiting = [(open_accs[i], tiles[i]) for i in range(OPEN_TILES)]
+                    tiles = tiles[OPEN_TILES:]
+            elif k - 2 >= PASSES:
+                g1 = k - 2 - PASSES
+                for j, n in tiles[:MXS]:
+                    acc = new_acc()
+                    for g in range(PASSES):
+                        multiply(acc, j, n, g)
+                    waiting.append((acc, (j, n)))
+                tiles = tiles[MXS:]
+                if g1 == 0:
+                    open_accs = [new_acc() for i in range(OPEN1)]
+                for i in range(OPEN1):
+                    multiply(open_accs[i], tiles1[i][0], tiles1[i][1], g1)
+        for j, n in tiles:
+            acc = new_acc()
             for g in range(PASSES):
-                multiply(acc, i, g)
-            finish(acc, i)
+                multiply(acc, j, n, g)
+            waiting.append((acc, (j, n)))
+        for acc, (j, n) in waiting:
+            finish(acc, j, n)
+        for i in range(OPEN1):
+            finish(open_accs[i], tiles1[i][0], tiles1[i][1])
+        for j, n in tiles1[OPEN1:]:
+            acc = new_acc()
+            for g in range(PASSES):
+                multiply(acc, j, n, g)
+            finish(acc, j, n)

@@ -28,9 +28,14 @@ N_HALVES = DM // N_TILE
 UNIT_TILES = 4
 UNIT_ROWS = UNIT_TILES * P
 HALVES = ROW_TILES // UNIT_TILES
-OPEN_TILES = 3
-OPEN1 = 3
-S_PLANES0 = 3
+OPEN_TILES = 1
+OPEN1 = 1
+GRAM0 = 0
+GRAM1 = 0
+H_B = 4
+W_B = 2
+A_B = 1
+S_PLANES0 = 2
 S_PLANES1 = 4
 W_S = 4
 EPIS = 2
@@ -50,11 +55,10 @@ def tile_mlstmblock_pb_kernel(tc, h_attn, gn_w, gn_b, W_out, x, skip_scale, out)
     with ExitStack() as ctx:
         ctx.enter_context(tc.manual_schedule())
         keep = ctx.enter_context(tc.tile_pool(name="keep", bufs=1))
-        small = ctx.enter_context(tc.tile_pool(name="small", bufs=2))
         stage = ctx.enter_context(tc.tile_pool(name="stage", bufs=3))
         results = ctx.enter_context(tc.tile_pool(name="results", bufs=4))
         stats_bank = ctx.enter_context(tc.psum_pool(name="stats_bank", bufs=1))
-        turned = ctx.enter_context(tc.psum_pool(name="turned", bufs=7))
+        turned = ctx.enter_context(tc.psum_pool(name="turned", bufs=1))
 
         gn_w_sb = keep.tile([P, PASSES, PACK], BF16)
         gn_b_sb = keep.tile([P, PASSES, PACK], BF16)
@@ -85,10 +89,8 @@ def tile_mlstmblock_pb_kernel(tc, h_attn, gn_w, gn_b, W_out, x, skip_scale, out)
         for u in range(GROUPS_PER_PASS):
             matrix = keep.tile([P, P], F32, name="mean_matrix%d" % u)
             nc.vector.memset(matrix[:], 0.0)
-            nc.vector.memset(matrix[:, u * half : (u + 1) * half], 1.0 / (S * GROUP))
+            nc.vector.memset(matrix[:, u * half : (u + 1) * half], -1.0 / (S * GROUP))
             mean_of.append(matrix)
-        minus_half = keep.tile([P, 1], F32)
-        nc.vector.memset(minus_half[:], -0.5)
 
         h_codes = keep.tile([P, PASSES, S], U32, align_bytes=64)
         h_scales = keep.tile([P, PASSES, S], U8, align_bytes=64)
@@ -100,6 +102,14 @@ def tile_mlstmblock_pb_kernel(tc, h_attn, gn_w, gn_b, W_out, x, skip_scale, out)
         gain = [keep.tile(quad, F32, name="gain%d" % g) for g in range(PASSES)]
         shift = [keep.tile(quad, F32, name="shift%d" % g) for g in range(PASSES)]
         skip = keep.tile([P, 1], F32)
+        moments = [keep.tile([P, 2], F32, name="moments%d" % g) for g in range(PASSES)]
+        negvar = [keep.tile([P, 1], F32, name="negvar%d" % g) for g in range(PASSES)]
+        sd = [keep.tile([P, 1], F32, name="sd%d" % g) for g in range(PASSES)]
+        eps = keep.tile([P, 1], F32)
+        nc.vector.memset(eps[:], 0.0)
+        nc.vector.tensor_scalar(out=eps[:], in0=eps[:], scalar1=EPS_GN, scalar2=None, op0=ALU.add)
+        nc.scalar.activation(out=sd[0][:], in_=eps[:], func=ACT.Sqrt)
+        rstd = [keep.tile([P, 1], F32, name="rstd%d" % g) for g in range(PASSES)]
 
         def sums(g):
             for u in range(GROUPS_PER_PASS):
@@ -129,6 +139,23 @@ def tile_mlstmblock_pb_kernel(tc, h_attn, gn_w, gn_b, W_out, x, skip_scale, out)
                 accum_out=part[g][:, u, 1:2],
             )
 
+        def gram(g, u):
+            bank = turned.tile([P, P], F32, tag="a", bufs=A_B, name="gram")
+            for j in range(ROW_TILES):
+                for c in range(2):
+                    chunk = h_raw[g][:, j, u * GROUP + c * P : u * GROUP + (c + 1) * P]
+                    nc.tensor.matmul(
+                        out=bank[:], lhsT=chunk, rhs=chunk, start=(j == 0 and c == 0), stop=(j == ROW_TILES - 1 and c == 1)
+                    )
+            return bank
+
+        def diagonal(g, u, bank):
+            scratch = stage.tile([P, P], F32, name="scratch_d")
+            nc.vector.scalar_tensor_tensor(
+                out=scratch[:], in0=bank[:], scalar=1.0, in1=ident_f32[:], op0=ALU.mult, op1=ALU.mult,
+                accum_out=part[g][:, u, 1:2],
+            )
+
         def totals(g):
             for u in range(GROUPS_PER_PASS):
                 nc.tensor.matmul(
@@ -136,25 +163,31 @@ def tile_mlstmblock_pb_kernel(tc, h_attn, gn_w, gn_b, W_out, x, skip_scale, out)
                     start=(u == 0), stop=(u == GROUPS_PER_PASS - 1),
                 )
 
+        def moments_of(g):
+            nc.vector.tensor_copy(out=moments[g][:], in_=stats_ps[:, g, 2:4])
+            nc.vector.scalar_tensor_tensor(
+                out=negvar[g][:], in0=moments[g][:, 0:1], scalar=moments[g][:, 0:1], in1=moments[g][:, 1:2],
+                op0=ALU.mult, op1=ALU.add,
+            )
+
+        def deviation(g):
+            nc.scalar.activation(out=sd[g][:], in_=negvar[g][:], func=ACT.Sqrt, scale=-1.0, bias=eps[:])
+
         def gain_and_shift(g):
-            moments = small.tile([P, 2], F32, name="moments")
-            nc.vector.tensor_copy(out=moments[:], in_=stats_ps[:, g, 2:4])
-            mean = moments[:, 0:1]
-            var = small.tile([P, 1], F32, name="var")
-            rstd = small.tile([P, 1], F32, name="rstd")
-            nc.gpsimd.tensor_tensor(out=var[:], in0=mean, in1=mean, op=ALU.mult)
-            nc.gpsimd.tensor_tensor(out=var[:], in0=moments[:, 1:2], in1=var[:], op=ALU.subtract)
-            nc.gpsimd.tensor_scalar(out=var[:], in0=var[:], scalar1=1.0, scalar2=EPS_GN, op0=ALU.mult, op1=ALU.add)
-            nc.gpsimd.tensor_tensor(out=rstd[:], in0=var[:], in1=minus_half[:], op=ALU.pow)
-            nc.gpsimd.tensor_tensor(out=gain[g][:], in0=gn_w_sb[:, g, :], in1=rstd[:].to_broadcast(quad), op=ALU.mult)
-            nc.gpsimd.tensor_tensor(out=shift[g][:], in0=gain[g][:], in1=mean.to_broadcast(quad), op=ALU.mult)
-            nc.gpsimd.tensor_tensor(out=shift[g][:], in0=gn_b_sb[:, g, :], in1=shift[g][:], op=ALU.subtract)
+            nc.vector.reciprocal(out=rstd[g][:], in_=sd[g][:])
+            nc.vector.tensor_scalar(
+                out=gain[g][:], in0=gn_w_sb[:, g, :], scalar1=rstd[g][:, 0:1], scalar2=None, op0=ALU.mult
+            )
+            nc.vector.scalar_tensor_tensor(
+                out=shift[g][:], in0=gain[g][:], scalar=moments[g][:, 0:1], in1=gn_b_sb[:, g, :],
+                op0=ALU.mult, op1=ALU.add,
+            )
 
         def transpose_h(g, r):
             words = h_raw[g][:].rearrange("p j c -> p (j c)").bitcast(F32).rearrange("p (j q u) -> p j u q", j=ROW_TILES, u=2)
             banks = []
             for u in range(2):
-                bank = turned.tile([P, UNIT_TILES, P], F32, tag="bank", name="hT")
+                bank = turned.tile([P, UNIT_TILES, P], F32, tag="h", bufs=H_B, name="hT")
                 for i in range(UNIT_TILES):
                     nc.tensor.transpose(out=bank[:, i, :], in_=words[:, r * UNIT_TILES + i, u, :], identity=ident_f32[:])
                 banks.append(bank)
@@ -195,18 +228,18 @@ def tile_mlstmblock_pb_kernel(tc, h_attn, gn_w, gn_b, W_out, x, skip_scale, out)
                 in_=grouped[:].rearrange("p s t -> p (s t)"),
             )
 
-        def transpose_w(g, scalar_copies):
-            grouped = stage.tile([P, DM * PACK], BF16, align_bytes=64, name="w_grouped")
+        def transpose_w(g, a):
+            bank = turned.tile([P, 2, 2, P], F32, tag="w", bufs=W_B, name="wT")
+            for c in range(2):
+                words = w_raw[g][:, 2 * a + c, :].bitcast(F32).rearrange("p (q u) -> p u q", u=2)
+                for u in range(2):
+                    nc.tensor.transpose(out=bank[:, c, u, :], in_=words[:, u, :], identity=ident_f32[:])
+            return bank
+
+        def copy_w(grouped, bank, a, on_scalar):
             grouped_words = grouped[:].bitcast(F32).rearrange("p (a c m u) -> p a c m u", a=W_TILES // 2, c=2, u=2)
-            for a in range(W_TILES // 2):
-                bank = turned.tile([P, 2, 2, P], F32, tag="bank", name="wT")
-                for c in range(2):
-                    words = w_raw[g][:, 2 * a + c, :].bitcast(F32).rearrange("p (q u) -> p u q", u=2)
-                    for u in range(2):
-                        nc.tensor.transpose(out=bank[:, c, u, :], in_=words[:, u, :], identity=ident_f32[:])
-                copy = nc.scalar.copy if a < scalar_copies else nc.vector.tensor_copy
-                copy(out=grouped_words[:, a], in_=bank[:].rearrange("p c u m -> p c m u"))
-            return grouped
+            copy = nc.scalar.copy if on_scalar else nc.vector.tensor_copy
+            copy(out=grouped_words[:, a], in_=bank[:].rearrange("p c u m -> p c m u"))
 
         def quantise_w(g, grouped):
             nc.vector.quantize_mx(out=w_codes[:, g, :].bitcast(FP8X4), scales=w_scales[:, g, :], in_=grouped[:])
@@ -228,78 +261,100 @@ def tile_mlstmblock_pb_kernel(tc, h_attn, gn_w, gn_b, W_out, x, skip_scale, out)
             )
             nc.sync.dma_start(out=out_rows[:, j, cols], in_=result[:])
 
-        def new_acc():
-            return turned.tile([P, N_TILE], F32, tag="bank", name="acc")
+        def new_acc(late=False):
+            if late:
+                flip.append(1)
+                if len(flip) % 2:
+                    return turned.tile([P, N_TILE], F32, tag="w", bufs=W_B, name="acc")
+            return turned.tile([P, N_TILE], F32, tag="a", bufs=A_B, name="acc")
+
+        flip = []
 
         tiles = [(j, n) for j in range(UNIT_TILES) for n in range(N_HALVES)]
         tiles1 = [(j, n) for j in range(UNIT_TILES, ROW_TILES) for n in range(N_HALVES)]
-        open_accs = []
-        hb = {}
-        wg = {}
-        pl = {}
-        gr = {}
         units = [(g, r) for r in range(HALVES) for g in range(PASSES)]
+        hb = {}
+        pl = {}
+        wg = {}
         waiting = []
         for k in range(len(units) + 2):
-            if k < PASSES:
-                squares_on_scalar(k, 0)
-            if 0 <= k - 2 < len(units):
-                g, r = units[k - 2]
-                gr[k - 2] = regroup(pl[k - 2])
-                if r == 0:
-                    quantise_w(g, wg[g])
-                else:
-                    for acc, (j, n) in waiting[:EPIS]:
-                        finish(acc, j, n)
-                    waiting = waiting[EPIS:]
-                quantise_h(g, r, gr[k - 2])
-            if k < PASSES:
-                squares_on_vector(k, 1)
+            stats = k < PASSES
+            if stats:
+                grams = [(u, gram(k, u)) for u in range(2) if k < (GRAM0, GRAM1)[u]]
+                if k >= GRAM0:
+                    squares_on_scalar(k, 0)
                 sums(k)
+                if k >= GRAM1:
+                    squares_on_vector(k, 1)
+                for u, bank in grams:
+                    diagonal(k, u, bank)
                 keep_sums(k)
+            last = k - 1
+            if 0 <= last < len(units):
+                pl[last] = stage.tile([P, PACK, UNIT_ROWS], BF16, name="planes")
+                sp = S_PLANES0 if units[last][1] == 0 else S_PLANES1
+                for t in range(PACK - 1, sp - 1, -1):
+                    normalise(units[last][0], hb[last], pl[last], t, False)
+            if 0 <= last < PASSES:
+                wg[last] = stage.tile([P, DM * PACK], BF16, align_bytes=64, name="w_grouped")
+                for a in range(2):
+                    copy_w(wg[last], transpose_w(last, a), a, a < W_S)
+            if stats:
+                totals(k)
+            if 0 <= k - 2 < len(units):
+                grouped = regroup(pl[k - 2])
+            if stats:
+                moments_of(k)
+                deviation(k)
+            if 0 <= last < PASSES:
+                for a in range(2, 4):
+                    copy_w(wg[last], transpose_w(last, a), a, a < W_S)
             if k < len(units):
                 hb[k] = transpose_h(units[k][0], units[k][1])
-            if 0 <= k - 1 < len(units):
-                g, r = units[k - 1]
-                pl[k - 1] = normalise_all(g, hb[k - 1], S_PLANES0 if r == 0 else S_PLANES1)
-                if r == 0:
-                    wg[g] = transpose_w(g, W_S)
-            if k < PASSES:
-                totals(k)
+            if 0 <= k - 2 < PASSES:
+                quantise_w(k - 2, wg[k - 2])
+            if stats:
                 gain_and_shift(k)
+            for acc, (j, n) in waiting[:EPIS]:
+                finish(acc, j, n)
+            waiting = waiting[EPIS:]
+            if 0 <= k - 2 < len(units):
+                quantise_h(units[k - 2][0], units[k - 2][1], grouped)
+            if 0 <= last < len(units):
+                for t in range(sp):
+                    normalise(units[last][0], hb[last], pl[last], t, True)
             if 0 <= k - 2 < PASSES:
                 g = k - 2
                 if g == 0:
-                    open_accs = [new_acc() for i in range(OPEN_TILES)]
+                    open0 = [new_acc() for i in range(OPEN_TILES)]
                 for i in range(OPEN_TILES):
-                    multiply(open_accs[i], tiles[i][0], tiles[i][1], g)
+                    multiply(open0[i], tiles[i][0], tiles[i][1], g)
                 if g == PASSES - 1:
                     nc.vector.tensor_copy(out=skip[:], in_=skip_bf[:])
-                    waiting = [(open_accs[i], tiles[i]) for i in range(OPEN_TILES)]
+                    waiting = [(open0[i], tiles[i]) for i in range(OPEN_TILES)]
                     tiles = tiles[OPEN_TILES:]
             elif k - 2 >= PASSES:
-                g1 = k - 2 - PASSES
                 for j, n in tiles[:MXS]:
-                    acc = new_acc()
+                    acc = new_acc(True)
                     for g in range(PASSES):
                         multiply(acc, j, n, g)
                     waiting.append((acc, (j, n)))
                 tiles = tiles[MXS:]
-                if g1 == 0:
-                    open_accs = [new_acc() for i in range(OPEN1)]
+                if k - 2 == PASSES:
+                    open1 = [new_acc(True) for i in range(OPEN1)]
                 for i in range(OPEN1):
-                    multiply(open_accs[i], tiles1[i][0], tiles1[i][1], g1)
+                    multiply(open1[i], tiles1[i][0], tiles1[i][1], k - 2 - PASSES)
         for j, n in tiles:
-            acc = new_acc()
+            acc = new_acc(True)
             for g in range(PASSES):
                 multiply(acc, j, n, g)
             waiting.append((acc, (j, n)))
         for acc, (j, n) in waiting:
             finish(acc, j, n)
         for i in range(OPEN1):
-            finish(open_accs[i], tiles1[i][0], tiles1[i][1])
+            finish(open1[i], tiles1[i][0], tiles1[i][1])
         for j, n in tiles1[OPEN1:]:
-            acc = new_acc()
+            acc = new_acc(True)
             for g in range(PASSES):
                 multiply(acc, j, n, g)
             finish(acc, j, n)

@@ -25,21 +25,19 @@ ROW_TILES = S // P
 W_TILES = DM // P
 N_TILE = 512
 N_HALVES = DM // N_TILE
-UNIT_TILES = 4
-UNIT_ROWS = UNIT_TILES * P
-HALVES = ROW_TILES // UNIT_TILES
-OPEN_TILES = 1
-OPEN1 = 1
-GRAM0 = 0
-GRAM1 = 0
-H_B = 4
-W_B = 2
-A_B = 1
-S_PLANES0 = 2
-S_PLANES1 = 4
-W_S = 4
-EPIS = 2
-MXS = 2
+GROUP_TILES = 2
+GROUP_ROWS = GROUP_TILES * P
+ROW_GROUPS = ROW_TILES // GROUP_TILES
+V_PLANES = 0
+W_V = (1,)
+W_V4 = (1, 3)
+H_B = 2
+W_B = 4
+RUN = 1
+E0 = 0
+E1 = 1
+E2 = 1
+E3 = 1
 LOADS = "h0 h1 w0 h2 w1 h3 w2 w3"
 
 FLOPS = 2 * S * DM * DI
@@ -57,7 +55,7 @@ def tile_mlstmblock_pb_kernel(tc, h_attn, gn_w, gn_b, W_out, x, skip_scale, out)
         keep = ctx.enter_context(tc.tile_pool(name="keep", bufs=1))
         stage = ctx.enter_context(tc.tile_pool(name="stage", bufs=3))
         results = ctx.enter_context(tc.tile_pool(name="results", bufs=4))
-        stats_bank = ctx.enter_context(tc.psum_pool(name="stats_bank", bufs=1))
+        planes_pool = ctx.enter_context(tc.tile_pool(name="planes_pool", bufs=6))
         turned = ctx.enter_context(tc.psum_pool(name="turned", bufs=1))
 
         gn_w_sb = keep.tile([P, PASSES, PACK], BF16)
@@ -92,11 +90,11 @@ def tile_mlstmblock_pb_kernel(tc, h_attn, gn_w, gn_b, W_out, x, skip_scale, out)
             nc.vector.memset(matrix[:, u * half : (u + 1) * half], -1.0 / (S * GROUP))
             mean_of.append(matrix)
 
-        h_codes = keep.tile([P, PASSES, S], U32, align_bytes=64)
-        h_scales = keep.tile([P, PASSES, S], U8, align_bytes=64)
+        h_codes = [keep.tile([P, PASSES * GROUP_ROWS], U32, align_bytes=64, name="h_codes%d" % m) for m in range(ROW_GROUPS)]
+        h_scales = [keep.tile([P, PASSES * GROUP_ROWS], U8, align_bytes=64, name="h_scales%d" % m) for m in range(ROW_GROUPS)]
         w_codes = keep.tile([P, PASSES, DM], U32, align_bytes=64)
         w_scales = keep.tile([P, PASSES, DM], U8, align_bytes=64)
-        stats_ps = stats_bank.tile([P, PASSES, 4], F32)
+        stats_ps = turned.tile([P, PASSES, 4], F32, tag="s", bufs=1, name="stats_ps")
         part = [keep.tile([P, GROUPS_PER_PASS, 2], F32, name="part%d" % g) for g in range(PASSES)]
         quad = [P, PACK]
         gain = [keep.tile(quad, F32, name="gain%d" % g) for g in range(PASSES)]
@@ -139,23 +137,6 @@ def tile_mlstmblock_pb_kernel(tc, h_attn, gn_w, gn_b, W_out, x, skip_scale, out)
                 accum_out=part[g][:, u, 1:2],
             )
 
-        def gram(g, u):
-            bank = turned.tile([P, P], F32, tag="a", bufs=A_B, name="gram")
-            for j in range(ROW_TILES):
-                for c in range(2):
-                    chunk = h_raw[g][:, j, u * GROUP + c * P : u * GROUP + (c + 1) * P]
-                    nc.tensor.matmul(
-                        out=bank[:], lhsT=chunk, rhs=chunk, start=(j == 0 and c == 0), stop=(j == ROW_TILES - 1 and c == 1)
-                    )
-            return bank
-
-        def diagonal(g, u, bank):
-            scratch = stage.tile([P, P], F32, name="scratch_d")
-            nc.vector.scalar_tensor_tensor(
-                out=scratch[:], in0=bank[:], scalar=1.0, in1=ident_f32[:], op0=ALU.mult, op1=ALU.mult,
-                accum_out=part[g][:, u, 1:2],
-            )
-
         def totals(g):
             for u in range(GROUPS_PER_PASS):
                 nc.tensor.matmul(
@@ -183,19 +164,20 @@ def tile_mlstmblock_pb_kernel(tc, h_attn, gn_w, gn_b, W_out, x, skip_scale, out)
                 op0=ALU.mult, op1=ALU.add,
             )
 
-        def transpose_h(g, r):
+        def transpose_h(m, g):
             words = h_raw[g][:].rearrange("p j c -> p (j c)").bitcast(F32).rearrange("p (j q u) -> p j u q", j=ROW_TILES, u=2)
-            banks = []
+            tag = "w" if m > 0 and g % 2 == 1 else "h"
+            bank = turned.tile([P, 2, GROUP_TILES, P], F32, tag=tag, bufs=W_B if tag == "w" else H_B, name="hT")
             for u in range(2):
-                bank = turned.tile([P, UNIT_TILES, P], F32, tag="h", bufs=H_B, name="hT")
-                for i in range(UNIT_TILES):
-                    nc.tensor.transpose(out=bank[:, i, :], in_=words[:, r * UNIT_TILES + i, u, :], identity=ident_f32[:])
-                banks.append(bank)
-            return banks
+                for i in range(GROUP_TILES):
+                    nc.tensor.transpose(
+                        out=bank[:, u, i, :], in_=words[:, m * GROUP_TILES + i, u, :], identity=ident_f32[:]
+                    )
+            return bank
 
-        def normalise(g, banks, planes, t, on_scalar):
+        def normalise(g, bank, planes, t, on_scalar):
             u, e = t // 2, t % 2
-            values = banks[u][:].rearrange("p i r -> p (i r)").bitcast(BF16).rearrange("p (r e) -> p e r", e=2)[:, e, :]
+            values = bank[:, u].rearrange("p i r -> p (i r)").bitcast(BF16).rearrange("p (r e) -> p e r", e=2)[:, e, :]
             if on_scalar:
                 nc.scalar.activation(
                     out=planes[:, t, :], in_=values, func=ACT.Identity,
@@ -207,25 +189,26 @@ def tile_mlstmblock_pb_kernel(tc, h_attn, gn_w, gn_b, W_out, x, skip_scale, out)
                     scalar2=shift[g][:, t : t + 1], op0=ALU.mult, op1=ALU.add,
                 )
 
-        def normalise_all(g, banks, scalar_planes):
-            planes = stage.tile([P, PACK, UNIT_ROWS], BF16, name="planes")
+        def normalise_all(g, bank):
+            planes = planes_pool.tile([P, PACK, GROUP_ROWS], BF16, name="planes")
             for t in range(PACK):
-                normalise(g, banks, planes, t, t < scalar_planes)
+                normalise(g, bank, planes, t, t >= V_PLANES)
             return planes
 
-        def regroup(planes):
-            grouped = stage.tile([P, UNIT_ROWS, PACK], BF16, align_bytes=64, name="h_grouped")
+        def regroup(g, planes, grouped):
             nc.vector.tensor_copy(
-                out=grouped[:].rearrange("p (c i) t -> p c t i", i=4),
+                out=grouped[:, g].rearrange("p (c i) t -> p c t i", i=4),
                 in_=planes[:].rearrange("p t (c i) -> p c t i", i=4),
             )
-            return grouped
 
-        def quantise_h(g, r, grouped):
-            rows = slice(r * UNIT_ROWS, (r + 1) * UNIT_ROWS)
+        def new_grouped():
+            return stage.tile([P, PASSES, GROUP_ROWS, PACK], BF16, align_bytes=64, name="h_grouped")
+
+        def quantise_h(m, g0, g1, grouped):
+            cols = slice(g0 * GROUP_ROWS, g1 * GROUP_ROWS)
             nc.vector.quantize_mx(
-                out=h_codes[:, g, rows].bitcast(FP8X4), scales=h_scales[:, g, rows],
-                in_=grouped[:].rearrange("p s t -> p (s t)"),
+                out=h_codes[m][:, cols].bitcast(FP8X4), scales=h_scales[m][:, cols],
+                in_=grouped[:, g0:g1].rearrange("p g s t -> p (g s t)"),
             )
 
         def transpose_w(g, a):
@@ -245,10 +228,11 @@ def tile_mlstmblock_pb_kernel(tc, h_attn, gn_w, gn_b, W_out, x, skip_scale, out)
             nc.vector.quantize_mx(out=w_codes[:, g, :].bitcast(FP8X4), scales=w_scales[:, g, :], in_=grouped[:])
 
         def multiply(acc, j, n, g):
-            rows = slice(j * P, (j + 1) * P)
+            m, i = j // GROUP_TILES, j % GROUP_TILES
+            rows = slice(g * GROUP_ROWS + i * P, g * GROUP_ROWS + (i + 1) * P)
             cols = slice(n * N_TILE, (n + 1) * N_TILE)
             nc.tensor.matmul_mx(
-                out=acc[:], lhsT=h_codes[:, g, rows].bitcast(FP8X4), lhsT_scale=h_scales[:, g, rows],
+                out=acc[:], lhsT=h_codes[m][:, rows].bitcast(FP8X4), lhsT_scale=h_scales[m][:, rows],
                 rhs=w_codes[:, g, cols].bitcast(FP8X4), rhs_scale=w_scales[:, g, cols],
                 start=(g == 0), stop=(g == PASSES - 1),
             )
@@ -261,100 +245,78 @@ def tile_mlstmblock_pb_kernel(tc, h_attn, gn_w, gn_b, W_out, x, skip_scale, out)
             )
             nc.sync.dma_start(out=out_rows[:, j, cols], in_=result[:])
 
-        def new_acc(late=False):
-            if late:
-                flip.append(1)
-                if len(flip) % 2:
-                    return turned.tile([P, N_TILE], F32, tag="w", bufs=W_B, name="acc")
-            return turned.tile([P, N_TILE], F32, tag="a", bufs=A_B, name="acc")
+        acc_tags = []
 
-        flip = []
+        def new_acc():
+            tag = ("a", "w", "s", "w")[len(acc_tags) % 4]
+            acc_tags.append(tag)
+            return turned.tile([P, N_TILE], F32, tag=tag, bufs=W_B if tag == "w" else 1, name="acc")
 
-        tiles = [(j, n) for j in range(UNIT_TILES) for n in range(N_HALVES)]
-        tiles1 = [(j, n) for j in range(UNIT_TILES, ROW_TILES) for n in range(N_HALVES)]
-        units = [(g, r) for r in range(HALVES) for g in range(PASSES)]
+        group_tiles = [[(m * GROUP_TILES + i, n) for i in range(GROUP_TILES) for n in range(N_HALVES)] for m in range(ROW_GROUPS)]
         hb = {}
         pl = {}
         wg = {}
-        waiting = []
-        for k in range(len(units) + 2):
+        hb1 = {}
+        pl1 = {}
+        grouped = {0: new_grouped()}
+        for k in range(PASSES + 2):
             stats = k < PASSES
-            if stats:
-                grams = [(u, gram(k, u)) for u in range(2) if k < (GRAM0, GRAM1)[u]]
-                if k >= GRAM0:
-                    squares_on_scalar(k, 0)
-                sums(k)
-                if k >= GRAM1:
-                    squares_on_vector(k, 1)
-                for u, bank in grams:
-                    diagonal(k, u, bank)
-                keep_sums(k)
             last = k - 1
-            if 0 <= last < len(units):
-                pl[last] = stage.tile([P, PACK, UNIT_ROWS], BF16, name="planes")
-                sp = S_PLANES0 if units[last][1] == 0 else S_PLANES1
-                for t in range(PACK - 1, sp - 1, -1):
-                    normalise(units[last][0], hb[last], pl[last], t, False)
+            if stats:
+                squares_on_scalar(k, 0)
+                sums(k)
+                squares_on_vector(k, 1)
+                keep_sums(k)
             if 0 <= last < PASSES:
+                pl[last] = normalise_all(last, hb[last])
                 wg[last] = stage.tile([P, DM * PACK], BF16, align_bytes=64, name="w_grouped")
                 for a in range(2):
-                    copy_w(wg[last], transpose_w(last, a), a, a < W_S)
+                    copy_w(wg[last], transpose_w(last, a), a, a not in (W_V if k < PASSES else W_V4))
             if stats:
                 totals(k)
-            if 0 <= k - 2 < len(units):
-                grouped = regroup(pl[k - 2])
             if stats:
                 moments_of(k)
                 deviation(k)
             if 0 <= last < PASSES:
+                regroup(last, pl[last], grouped[0])
                 for a in range(2, 4):
-                    copy_w(wg[last], transpose_w(last, a), a, a < W_S)
-            if k < len(units):
-                hb[k] = transpose_h(units[k][0], units[k][1])
-            if 0 <= k - 2 < PASSES:
-                quantise_w(k - 2, wg[k - 2])
+                    copy_w(wg[last], transpose_w(last, a), a, a not in (W_V if k < PASSES else W_V4))
             if stats:
                 gain_and_shift(k)
-            for acc, (j, n) in waiting[:EPIS]:
-                finish(acc, j, n)
-            waiting = waiting[EPIS:]
-            if 0 <= k - 2 < len(units):
-                quantise_h(units[k - 2][0], units[k - 2][1], grouped)
-            if 0 <= last < len(units):
-                for t in range(sp):
-                    normalise(units[last][0], hb[last], pl[last], t, True)
+                hb[k] = transpose_h(0, k)
+            if k == PASSES:
+                for g in range(PASSES):
+                    hb1[g] = transpose_h(1, g)
+                    pl1[g] = normalise_all(g, hb1[g])
             if 0 <= k - 2 < PASSES:
-                g = k - 2
-                if g == 0:
-                    open0 = [new_acc() for i in range(OPEN_TILES)]
-                for i in range(OPEN_TILES):
-                    multiply(open0[i], tiles[i][0], tiles[i][1], g)
-                if g == PASSES - 1:
-                    nc.vector.tensor_copy(out=skip[:], in_=skip_bf[:])
-                    waiting = [(open0[i], tiles[i]) for i in range(OPEN_TILES)]
-                    tiles = tiles[OPEN_TILES:]
-            elif k - 2 >= PASSES:
-                for j, n in tiles[:MXS]:
-                    acc = new_acc(True)
-                    for g in range(PASSES):
-                        multiply(acc, j, n, g)
-                    waiting.append((acc, (j, n)))
-                tiles = tiles[MXS:]
-                if k - 2 == PASSES:
-                    open1 = [new_acc(True) for i in range(OPEN1)]
-                for i in range(OPEN1):
-                    multiply(open1[i], tiles1[i][0], tiles1[i][1], k - 2 - PASSES)
-        for j, n in tiles:
-            acc = new_acc(True)
-            for g in range(PASSES):
-                multiply(acc, j, n, g)
-            waiting.append((acc, (j, n)))
-        for acc, (j, n) in waiting:
-            finish(acc, j, n)
-        for i in range(OPEN1):
-            finish(open1[i], tiles1[i][0], tiles1[i][1])
-        for j, n in tiles1[OPEN1:]:
-            acc = new_acc(True)
-            for g in range(PASSES):
-                multiply(acc, j, n, g)
+                quantise_w(k - 2, wg[k - 2])
+            if 0 <= last < PASSES:
+                quantise_h(0, last, last + 1, grouped[0])
+        nc.vector.tensor_copy(out=skip[:], in_=skip_bf[:])
+        waiting = []
+        for m in range(1, ROW_GROUPS + 1):
+            if m < ROW_GROUPS:
+                grouped[m] = new_grouped()
+            done_tiles = group_tiles[m - 1]
+            for s in range(PASSES):
+                if m + 1 < ROW_GROUPS and s % RUN == 0:
+                    for r in range(RUN):
+                        hb1[s + r] = transpose_h(m + 1, s + r)
+                if m < ROW_GROUPS:
+                    regroup(s, pl1[s], grouped[m])
+                if m + 1 < ROW_GROUPS:
+                    pl1[s] = normalise_all(s, hb1[s])
+                j, n = done_tiles[s]
+                acc = new_acc()
+                for g in range(PASSES):
+                    multiply(acc, j, n, g)
+                waiting.append((acc, j, n))
+                for i in range((E0, E1, E2, E3)[s] if m < ROW_GROUPS else 1):
+                    if len(waiting) > 0:
+                        acc, j, n = waiting[0]
+                        waiting.remove(waiting[0])
+                        finish(acc, j, n)
+            if m < ROW_GROUPS:
+                quantise_h(m, 0, PASSES, grouped[m])
+        for acc, j, n in waiting:
             finish(acc, j, n)

@@ -28,16 +28,13 @@ N_HALVES = DM // N_TILE
 GROUP_TILES = 2
 GROUP_ROWS = GROUP_TILES * P
 ROW_GROUPS = ROW_TILES // GROUP_TILES
-V_PLANES = 0
 W_V = (1,)
 W_V4 = (1, 3)
 H_B = 2
 W_B = 4
-RUN = 1
-E0 = 0
-E1 = 1
-E2 = 1
-E3 = 1
+RUN = 2
+ACC_TAGS = ("a", "w", "s", "w")
+PIECES0 = 2
 LOADS = "h0 h1 w0 h2 w1 h3 w2 w3"
 
 FLOPS = 2 * S * DM * DI
@@ -54,7 +51,7 @@ def tile_mlstmblock_pb_kernel(tc, h_attn, gn_w, gn_b, W_out, x, skip_scale, out)
         ctx.enter_context(tc.manual_schedule())
         keep = ctx.enter_context(tc.tile_pool(name="keep", bufs=1))
         stage = ctx.enter_context(tc.tile_pool(name="stage", bufs=3))
-        results = ctx.enter_context(tc.tile_pool(name="results", bufs=4))
+        results = ctx.enter_context(tc.tile_pool(name="results", bufs=8))
         planes_pool = ctx.enter_context(tc.tile_pool(name="planes_pool", bufs=6))
         turned = ctx.enter_context(tc.psum_pool(name="turned", bufs=1))
 
@@ -67,7 +64,11 @@ def tile_mlstmblock_pb_kernel(tc, h_attn, gn_w, gn_b, W_out, x, skip_scale, out)
         first = True
         for item in LOADS.split(" "):
             g = int(item[1])
-            if item[0] == "h":
+            if item == "h0" and PIECES0 > 1:
+                for i in range(PIECES0):
+                    rows = slice(i * ROW_TILES // PIECES0, (i + 1) * ROW_TILES // PIECES0)
+                    nc.sync.dma_start(out=h_raw[g][:, rows, :], in_=h_rows[:, rows, g * K_PASS : (g + 1) * K_PASS])
+            elif item[0] == "h":
                 nc.sync.dma_start(out=h_raw[g][:], in_=h_rows[:, :, g * K_PASS : (g + 1) * K_PASS])
             else:
                 nc.sync.dma_start(out=w_raw[g][:], in_=w_rows[:, :, g * K_PASS : (g + 1) * K_PASS])
@@ -96,18 +97,22 @@ def tile_mlstmblock_pb_kernel(tc, h_attn, gn_w, gn_b, W_out, x, skip_scale, out)
         w_scales = keep.tile([P, PASSES, DM], U8, align_bytes=64)
         stats_ps = turned.tile([P, PASSES, 4], F32, tag="s", bufs=1, name="stats_ps")
         part = [keep.tile([P, GROUPS_PER_PASS, 2], F32, name="part%d" % g) for g in range(PASSES)]
+        part0 = [part[0]]
+        for i in range(1, PIECES0):
+            extra = keep.tile([P, GROUPS_PER_PASS, 2], F32, name="part0_%d" % i)
+            nc.vector.memset(extra[:], 0.0)
+            part0.append(extra)
         quad = [P, PACK]
         gain = [keep.tile(quad, F32, name="gain%d" % g) for g in range(PASSES)]
         shift = [keep.tile(quad, F32, name="shift%d" % g) for g in range(PASSES)]
         skip = keep.tile([P, 1], F32)
         moments = [keep.tile([P, 2], F32, name="moments%d" % g) for g in range(PASSES)]
         negvar = [keep.tile([P, 1], F32, name="negvar%d" % g) for g in range(PASSES)]
-        sd = [keep.tile([P, 1], F32, name="sd%d" % g) for g in range(PASSES)]
         eps = keep.tile([P, 1], F32)
         nc.vector.memset(eps[:], 0.0)
         nc.vector.tensor_scalar(out=eps[:], in0=eps[:], scalar1=EPS_GN, scalar2=None, op0=ALU.add)
-        nc.scalar.activation(out=sd[0][:], in_=eps[:], func=ACT.Sqrt)
         rstd = [keep.tile([P, 1], F32, name="rstd%d" % g) for g in range(PASSES)]
+        nc.scalar.activation(out=rstd[0][:], in_=eps[:], func=ACT.Abs_reciprocal_sqrt)
 
         def sums(g):
             for u in range(GROUPS_PER_PASS):
@@ -123,42 +128,50 @@ def tile_mlstmblock_pb_kernel(tc, h_attn, gn_w, gn_b, W_out, x, skip_scale, out)
             nc.vector.tensor_copy(out=part[g][:, :, 0], in_=stats_ps[:, g, 0:2])
 
         def squares_on_scalar(g, u):
-            scratch = stage.tile([P, ROW_TILES, GROUP], BF16, name="scratch_s")
-            nc.scalar.activation(
-                out=scratch[:], in_=h_raw[g][:, :, u * GROUP : (u + 1) * GROUP], func=ACT.Square,
-                accum_out=part[g][:, u, 1:2],
-            )
-
-        def squares_on_vector(g, u):
-            group = h_raw[g][:, :, u * GROUP : (u + 1) * GROUP]
-            scratch = stage.tile([P, ROW_TILES, GROUP], BF16, name="scratch_v")
-            nc.vector.scalar_tensor_tensor(
-                out=scratch[:], in0=group, scalar=1.0, in1=group, op0=ALU.mult, op1=ALU.mult,
-                accum_out=part[g][:, u, 1:2],
-            )
-
-        def totals(g):
-            for u in range(GROUPS_PER_PASS):
-                nc.tensor.matmul(
-                    out=stats_ps[:, g, 2:4], lhsT=mean_of[u][:], rhs=part[g][:, u, :],
-                    start=(u == 0), stop=(u == GROUPS_PER_PASS - 1),
+            parts = part0 if g == 0 else [part[g]]
+            step = ROW_TILES // len(parts)
+            for i, sums_of in enumerate(parts):
+                scratch = stage.tile([P, ROW_TILES, GROUP], BF16, name="scratch_s")
+                nc.scalar.activation(
+                    out=scratch[:, 0:step, :], in_=h_raw[g][:, i * step : (i + 1) * step, u * GROUP : (u + 1) * GROUP], func=ACT.Square,
+                    accum_out=sums_of[:, u, 1:2],
                 )
 
-        def moments_of(g):
+        def squares_on_vector(g, u):
+            parts = part0 if g == 0 else [part[g]]
+            step = ROW_TILES // len(parts)
+            for i, sums_of in enumerate(parts):
+                group = h_raw[g][:, i * step : (i + 1) * step, u * GROUP : (u + 1) * GROUP]
+                scratch = stage.tile([P, ROW_TILES, GROUP], BF16, name="scratch_v")
+                nc.vector.scalar_tensor_tensor(
+                    out=scratch[:, 0:step, :], in0=group, scalar=1.0, in1=group, op0=ALU.mult, op1=ALU.mult,
+                    accum_out=sums_of[:, u, 1:2],
+                )
+
+        def totals(g):
+            terms = [(u, sums_of) for u in range(GROUPS_PER_PASS) for sums_of in (part0 if g == 0 else [part[g]])]
+            for i, (u, sums_of) in enumerate(terms):
+                nc.tensor.matmul(
+                    out=stats_ps[:, g, 2:4], lhsT=mean_of[u][:], rhs=sums_of[:, u, :],
+                    start=(i == 0), stop=(i == len(terms) - 1),
+                )
+
+        def keep_moments(g):
             nc.vector.tensor_copy(out=moments[g][:], in_=stats_ps[:, g, 2:4])
+
+        def negative_variance(g):
             nc.vector.scalar_tensor_tensor(
                 out=negvar[g][:], in0=moments[g][:, 0:1], scalar=moments[g][:, 0:1], in1=moments[g][:, 1:2],
                 op0=ALU.mult, op1=ALU.add,
             )
 
-        def deviation(g):
-            nc.scalar.activation(out=sd[g][:], in_=negvar[g][:], func=ACT.Sqrt, scale=-1.0, bias=eps[:])
-
-        def gain_and_shift(g):
-            nc.vector.reciprocal(out=rstd[g][:], in_=sd[g][:])
-            nc.vector.tensor_scalar(
-                out=gain[g][:], in0=gn_w_sb[:, g, :], scalar1=rstd[g][:, 0:1], scalar2=None, op0=ALU.mult
+        def gain_of(g):
+            nc.scalar.activation(
+                out=rstd[g][:], in_=negvar[g][:], func=ACT.Abs_reciprocal_sqrt, scale=-1.0, bias=eps[:]
             )
+            nc.scalar.activation(out=gain[g][:], in_=gn_w_sb[:, g, :], func=ACT.Identity, scale=rstd[g][:, 0:1])
+
+        def shift_of(g):
             nc.vector.scalar_tensor_tensor(
                 out=shift[g][:], in0=gain[g][:], scalar=moments[g][:, 0:1], in1=gn_b_sb[:, g, :],
                 op0=ALU.mult, op1=ALU.add,
@@ -166,8 +179,8 @@ def tile_mlstmblock_pb_kernel(tc, h_attn, gn_w, gn_b, W_out, x, skip_scale, out)
 
         def transpose_h(m, g):
             words = h_raw[g][:].rearrange("p j c -> p (j c)").bitcast(F32).rearrange("p (j q u) -> p j u q", j=ROW_TILES, u=2)
-            tag = "w" if m > 0 and g % 2 == 1 else "h"
-            bank = turned.tile([P, 2, GROUP_TILES, P], F32, tag=tag, bufs=W_B if tag == "w" else H_B, name="hT")
+            tag = "a" if m == 1 and g == 0 else ("w" if m > 0 and g % 2 == 1 else "h")
+            bank = turned.tile([P, 2, GROUP_TILES, P], F32, tag=tag, bufs={"w": W_B, "h": H_B}.get(tag, 1), name="hT")
             for u in range(2):
                 for i in range(GROUP_TILES):
                     nc.tensor.transpose(
@@ -192,11 +205,12 @@ def tile_mlstmblock_pb_kernel(tc, h_attn, gn_w, gn_b, W_out, x, skip_scale, out)
         def normalise_all(g, bank):
             planes = planes_pool.tile([P, PACK, GROUP_ROWS], BF16, name="planes")
             for t in range(PACK):
-                normalise(g, bank, planes, t, t >= V_PLANES)
+                normalise(g, bank, planes, t, True)
             return planes
 
-        def regroup(g, planes, grouped):
-            nc.vector.tensor_copy(
+        def regroup(g, planes, grouped, on_scalar):
+            copy = nc.scalar.copy if on_scalar else nc.vector.tensor_copy
+            copy(
                 out=grouped[:, g].rearrange("p (c i) t -> p c t i", i=4),
                 in_=planes[:].rearrange("p t (c i) -> p c t i", i=4),
             )
@@ -237,7 +251,15 @@ def tile_mlstmblock_pb_kernel(tc, h_attn, gn_w, gn_b, W_out, x, skip_scale, out)
                 start=(g == 0), stop=(g == PASSES - 1),
             )
 
-        def finish(acc, j, n):
+        def multiply_tile(j, n, waiting):
+            acc = new_acc()
+            for g in range(PASSES):
+                multiply(acc, j, n, g)
+            waiting.append((acc, j, n))
+
+        def finish(waiting):
+            acc, j, n = waiting[0]
+            waiting.remove(waiting[0])
             cols = slice(n * N_TILE, (n + 1) * N_TILE)
             result = results.tile([P, N_TILE], F32, name="result")
             nc.vector.scalar_tensor_tensor(
@@ -247,76 +269,83 @@ def tile_mlstmblock_pb_kernel(tc, h_attn, gn_w, gn_b, W_out, x, skip_scale, out)
 
         acc_tags = []
 
+        def new_w_grouped():
+            return stage.tile([P, DM * PACK], BF16, align_bytes=64, name="w_grouped")
+
+        def move_w(g, a):
+            copy_w(wg[g], transpose_w(g, a), a, a not in (W_V if g < PASSES - 1 else W_V4))
+
         def new_acc():
-            tag = ("a", "w", "s", "w")[len(acc_tags) % 4]
+            tag = ACC_TAGS[len(acc_tags) % len(ACC_TAGS)]
             acc_tags.append(tag)
             return turned.tile([P, N_TILE], F32, tag=tag, bufs=W_B if tag == "w" else 1, name="acc")
 
-        group_tiles = [[(m * GROUP_TILES + i, n) for i in range(GROUP_TILES) for n in range(N_HALVES)] for m in range(ROW_GROUPS)]
         hb = {}
         pl = {}
         wg = {}
         hb1 = {}
         pl1 = {}
-        grouped = {0: new_grouped()}
+        grouped = {0: new_grouped(), 1: new_grouped()}
         for k in range(PASSES + 2):
-            stats = k < PASSES
-            last = k - 1
-            if stats:
-                squares_on_scalar(k, 0)
-                sums(k)
+            now, last, older = k < PASSES, 0 <= k - 1 < PASSES, 0 <= k - 2 < PASSES
+            if now:
                 squares_on_vector(k, 1)
+                sums(k)
+                squares_on_scalar(k, 0)
+            if last:
+                pl[k - 1] = normalise_all(k - 1, hb[k - 1])
+            if now:
                 keep_sums(k)
-            if 0 <= last < PASSES:
-                pl[last] = normalise_all(last, hb[last])
-                wg[last] = stage.tile([P, DM * PACK], BF16, align_bytes=64, name="w_grouped")
-                for a in range(2):
-                    copy_w(wg[last], transpose_w(last, a), a, a not in (W_V if k < PASSES else W_V4))
-            if stats:
+            if last:
+                wg[k - 1] = new_w_grouped()
+                move_w(k - 1, 0)
+                move_w(k - 1, 1)
+            if now:
                 totals(k)
-            if stats:
-                moments_of(k)
-                deviation(k)
-            if 0 <= last < PASSES:
-                regroup(last, pl[last], grouped[0])
-                for a in range(2, 4):
-                    copy_w(wg[last], transpose_w(last, a), a, a not in (W_V if k < PASSES else W_V4))
-            if stats:
-                gain_and_shift(k)
+                keep_moments(k)
+            if last:
+                move_w(k - 1, 2)
+            if now:
                 hb[k] = transpose_h(0, k)
+            if older:
+                quantise_w(k - 2, wg[k - 2])
+            if now:
+                negative_variance(k)
+            if last:
+                regroup(k - 1, pl[k - 1], grouped[0], False)
+            if now:
+                gain_of(k)
+            if last:
+                move_w(k - 1, 3)
+            if now:
+                shift_of(k)
             if k == PASSES:
                 for g in range(PASSES):
-                    hb1[g] = transpose_h(1, g)
+                    if g > 0:
+                        hb1[g] = transpose_h(1, g)
                     pl1[g] = normalise_all(g, hb1[g])
-            if 0 <= k - 2 < PASSES:
-                quantise_w(k - 2, wg[k - 2])
-            if 0 <= last < PASSES:
-                quantise_h(0, last, last + 1, grouped[0])
+            if last:
+                quantise_h(0, k - 1, k, grouped[0])
+            if k == 2:
+                hb1[0] = transpose_h(1, 0)
         nc.vector.tensor_copy(out=skip[:], in_=skip_bf[:])
+
         waiting = []
         for m in range(1, ROW_GROUPS + 1):
-            if m < ROW_GROUPS:
+            if 1 < m < ROW_GROUPS:
                 grouped[m] = new_grouped()
-            done_tiles = group_tiles[m - 1]
             for s in range(PASSES):
                 if m + 1 < ROW_GROUPS and s % RUN == 0:
-                    for r in range(RUN):
-                        hb1[s + r] = transpose_h(m + 1, s + r)
+                    for g in range(s, s + RUN):
+                        hb1[g] = transpose_h(m + 1, g)
                 if m < ROW_GROUPS:
-                    regroup(s, pl1[s], grouped[m])
+                    regroup(s, pl1[s], grouped[m], m == ROW_GROUPS - 1 and s % 2 == 1)
+                    if s == PASSES - 1:
+                        quantise_h(m, 0, PASSES, grouped[m])
+                if len(waiting) > (1 if m < ROW_GROUPS else 0):
+                    finish(waiting)
                 if m + 1 < ROW_GROUPS:
                     pl1[s] = normalise_all(s, hb1[s])
-                j, n = done_tiles[s]
-                acc = new_acc()
-                for g in range(PASSES):
-                    multiply(acc, j, n, g)
-                waiting.append((acc, j, n))
-                for i in range((E0, E1, E2, E3)[s] if m < ROW_GROUPS else 1):
-                    if len(waiting) > 0:
-                        acc, j, n = waiting[0]
-                        waiting.remove(waiting[0])
-                        finish(acc, j, n)
-            if m < ROW_GROUPS:
-                quantise_h(m, 0, PASSES, grouped[m])
-        for acc, j, n in waiting:
-            finish(acc, j, n)
+                multiply_tile((m - 1) * GROUP_TILES + s // N_HALVES, s % N_HALVES, waiting)
+        for i in range(len(waiting)):
+            finish(waiting)

@@ -34,7 +34,6 @@ H_B = 2
 W_B = 4
 RUN = 2
 ACC_TAGS = ("a", "w", "s", "w")
-PIECES0 = 2
 LOADS = "h0 h1 w0 h2 w1 h3 w2 w3"
 
 FLOPS = 2 * S * DM * DI
@@ -64,9 +63,9 @@ def tile_mlstmblock_pb_kernel(tc, h_attn, gn_w, gn_b, W_out, x, skip_scale, out)
         first = True
         for item in LOADS.split(" "):
             g = int(item[1])
-            if item == "h0" and PIECES0 > 1:
-                for i in range(PIECES0):
-                    rows = slice(i * ROW_TILES // PIECES0, (i + 1) * ROW_TILES // PIECES0)
+            if item == "h0":
+                for i in range(2):
+                    rows = slice(i * ROW_TILES // 2, (i + 1) * ROW_TILES // 2)
                     nc.sync.dma_start(out=h_raw[g][:, rows, :], in_=h_rows[:, rows, g * K_PASS : (g + 1) * K_PASS])
             elif item[0] == "h":
                 nc.sync.dma_start(out=h_raw[g][:], in_=h_rows[:, :, g * K_PASS : (g + 1) * K_PASS])
@@ -83,25 +82,18 @@ def tile_mlstmblock_pb_kernel(tc, h_attn, gn_w, gn_b, W_out, x, skip_scale, out)
         make_identity(nc, ident_f32[:])
         ones = keep.tile([P, 1], BF16)
         nc.vector.memset(ones[:], 1.0)
-        mean_of = []
-        half = P // GROUPS_PER_PASS
-        for u in range(GROUPS_PER_PASS):
-            matrix = keep.tile([P, P], F32, name="mean_matrix%d" % u)
-            nc.vector.memset(matrix[:], 0.0)
-            nc.vector.memset(matrix[:, u * half : (u + 1) * half], -1.0 / (S * GROUP))
-            mean_of.append(matrix)
+        minus_mean_of = keep.tile([P, P], F32)
+        nc.vector.memset(minus_mean_of[:], -1.0 / (S * GROUP))
 
         h_codes = [keep.tile([P, PASSES * GROUP_ROWS], U32, align_bytes=64, name="h_codes%d" % m) for m in range(ROW_GROUPS)]
         h_scales = [keep.tile([P, PASSES * GROUP_ROWS], U8, align_bytes=64, name="h_scales%d" % m) for m in range(ROW_GROUPS)]
         w_codes = keep.tile([P, PASSES, DM], U32, align_bytes=64)
         w_scales = keep.tile([P, PASSES, DM], U8, align_bytes=64)
-        stats_ps = turned.tile([P, PASSES, 4], F32, tag="s", bufs=1, name="stats_ps")
+        stats_ps = turned.tile([P, PASSES, 6], F32, tag="s", bufs=1, name="stats_ps")
         part = [keep.tile([P, GROUPS_PER_PASS, 2], F32, name="part%d" % g) for g in range(PASSES)]
-        part0 = [part[0]]
-        for i in range(1, PIECES0):
-            extra = keep.tile([P, GROUPS_PER_PASS, 2], F32, name="part0_%d" % i)
-            nc.vector.memset(extra[:], 0.0)
-            part0.append(extra)
+        late_part0 = keep.tile([P, GROUPS_PER_PASS, 2], F32)
+        nc.vector.memset(late_part0[:], 0.0)
+        parts_of = [[part[0], late_part0]] + [[part[g]] for g in range(1, PASSES)]
         quad = [P, PACK]
         gain = [keep.tile(quad, F32, name="gain%d" % g) for g in range(PASSES)]
         shift = [keep.tile(quad, F32, name="shift%d" % g) for g in range(PASSES)]
@@ -128,7 +120,7 @@ def tile_mlstmblock_pb_kernel(tc, h_attn, gn_w, gn_b, W_out, x, skip_scale, out)
             nc.vector.tensor_copy(out=part[g][:, :, 0], in_=stats_ps[:, g, 0:2])
 
         def squares_on_scalar(g, u):
-            parts = part0 if g == 0 else [part[g]]
+            parts = parts_of[g]
             step = ROW_TILES // len(parts)
             for i, sums_of in enumerate(parts):
                 scratch = stage.tile([P, ROW_TILES, GROUP], BF16, name="scratch_s")
@@ -138,7 +130,7 @@ def tile_mlstmblock_pb_kernel(tc, h_attn, gn_w, gn_b, W_out, x, skip_scale, out)
                 )
 
         def squares_on_vector(g, u):
-            parts = part0 if g == 0 else [part[g]]
+            parts = parts_of[g]
             step = ROW_TILES // len(parts)
             for i, sums_of in enumerate(parts):
                 group = h_raw[g][:, i * step : (i + 1) * step, u * GROUP : (u + 1) * GROUP]
@@ -149,15 +141,17 @@ def tile_mlstmblock_pb_kernel(tc, h_attn, gn_w, gn_b, W_out, x, skip_scale, out)
                 )
 
         def totals(g):
-            terms = [(u, sums_of) for u in range(GROUPS_PER_PASS) for sums_of in (part0 if g == 0 else [part[g]])]
-            for i, (u, sums_of) in enumerate(terms):
+            for i, sums_of in enumerate(parts_of[g]):
                 nc.tensor.matmul(
-                    out=stats_ps[:, g, 2:4], lhsT=mean_of[u][:], rhs=sums_of[:, u, :],
-                    start=(i == 0), stop=(i == len(terms) - 1),
+                    out=stats_ps[:, g, 2:6], lhsT=minus_mean_of[:], rhs=sums_of[:].rearrange("p u k -> p (u k)"),
+                    start=(i == 0), stop=(i == len(parts_of[g]) - 1),
                 )
 
         def keep_moments(g):
-            nc.vector.tensor_copy(out=moments[g][:], in_=stats_ps[:, g, 2:4])
+            half = P // GROUPS_PER_PASS
+            for u in range(GROUPS_PER_PASS):
+                channels = slice(u * half, (u + 1) * half)
+                nc.vector.tensor_copy(out=moments[g][channels, :], in_=stats_ps[channels, g, 2 + 2 * u : 4 + 2 * u])
 
         def negative_variance(g):
             nc.vector.scalar_tensor_tensor(
@@ -241,27 +235,26 @@ def tile_mlstmblock_pb_kernel(tc, h_attn, gn_w, gn_b, W_out, x, skip_scale, out)
         def quantise_w(g, grouped):
             nc.vector.quantize_mx(out=w_codes[:, g, :].bitcast(FP8X4), scales=w_scales[:, g, :], in_=grouped[:])
 
-        def multiply(acc, j, n, g):
+        def multiply(acc, j, cols, g):
             m, i = j // GROUP_TILES, j % GROUP_TILES
             rows = slice(g * GROUP_ROWS + i * P, g * GROUP_ROWS + (i + 1) * P)
-            cols = slice(n * N_TILE, (n + 1) * N_TILE)
             nc.tensor.matmul_mx(
                 out=acc[:], lhsT=h_codes[m][:, rows].bitcast(FP8X4), lhsT_scale=h_scales[m][:, rows],
                 rhs=w_codes[:, g, cols].bitcast(FP8X4), rhs_scale=w_scales[:, g, cols],
                 start=(g == 0), stop=(g == PASSES - 1),
             )
 
-        def multiply_tile(j, n, waiting):
-            acc = new_acc()
+        def multiply_tile(j, c0, width, waiting):
+            acc = new_acc(width)
+            cols = slice(c0, c0 + width)
             for g in range(PASSES):
-                multiply(acc, j, n, g)
-            waiting.append((acc, j, n))
+                multiply(acc, j, cols, g)
+            waiting.append((acc, j, cols, width))
 
         def finish(waiting):
-            acc, j, n = waiting[0]
+            acc, j, cols, width = waiting[0]
             waiting.remove(waiting[0])
-            cols = slice(n * N_TILE, (n + 1) * N_TILE)
-            result = results.tile([P, N_TILE], F32, name="result")
+            result = results.tile([P, width], F32, name="result")
             nc.vector.scalar_tensor_tensor(
                 out=result[:], in0=x_sb[:, j, cols], scalar=skip[:, 0:1], in1=acc[:], op0=ALU.mult, op1=ALU.add
             )
@@ -275,10 +268,10 @@ def tile_mlstmblock_pb_kernel(tc, h_attn, gn_w, gn_b, W_out, x, skip_scale, out)
         def move_w(g, a):
             copy_w(wg[g], transpose_w(g, a), a, a not in (W_V if g < PASSES - 1 else W_V4))
 
-        def new_acc():
+        def new_acc(width):
             tag = ACC_TAGS[len(acc_tags) % len(ACC_TAGS)]
             acc_tags.append(tag)
-            return turned.tile([P, N_TILE], F32, tag=tag, bufs=W_B if tag == "w" else 1, name="acc")
+            return turned.tile([P, width], F32, tag=tag, bufs=W_B if tag == "w" else 1, name="acc")
 
         hb = {}
         pl = {}
@@ -296,6 +289,7 @@ def tile_mlstmblock_pb_kernel(tc, h_attn, gn_w, gn_b, W_out, x, skip_scale, out)
                 pl[k - 1] = normalise_all(k - 1, hb[k - 1])
             if now:
                 keep_sums(k)
+                hb[k] = transpose_h(0, k)
             if last:
                 wg[k - 1] = new_w_grouped()
                 move_w(k - 1, 0)
@@ -305,8 +299,6 @@ def tile_mlstmblock_pb_kernel(tc, h_attn, gn_w, gn_b, W_out, x, skip_scale, out)
                 keep_moments(k)
             if last:
                 move_w(k - 1, 2)
-            if now:
-                hb[k] = transpose_h(0, k)
             if older:
                 quantise_w(k - 2, wg[k - 2])
             if now:
@@ -319,13 +311,13 @@ def tile_mlstmblock_pb_kernel(tc, h_attn, gn_w, gn_b, W_out, x, skip_scale, out)
                 move_w(k - 1, 3)
             if now:
                 shift_of(k)
+            if last:
+                quantise_h(0, k - 1, k, grouped[0])
             if k == PASSES:
                 for g in range(PASSES):
                     if g > 0:
                         hb1[g] = transpose_h(1, g)
                     pl1[g] = normalise_all(g, hb1[g])
-            if last:
-                quantise_h(0, k - 1, k, grouped[0])
             if k == 2:
                 hb1[0] = transpose_h(1, 0)
         nc.vector.tensor_copy(out=skip[:], in_=skip_bf[:])
@@ -346,6 +338,12 @@ def tile_mlstmblock_pb_kernel(tc, h_attn, gn_w, gn_b, W_out, x, skip_scale, out)
                     finish(waiting)
                 if m + 1 < ROW_GROUPS:
                     pl1[s] = normalise_all(s, hb1[s])
-                multiply_tile((m - 1) * GROUP_TILES + s // N_HALVES, s % N_HALVES, waiting)
+                j, c0 = (m - 1) * GROUP_TILES + s // N_HALVES, s % N_HALVES * N_TILE
+                if m == ROW_GROUPS and s == PASSES - 1:
+                    multiply_tile(j, c0, N_TILE // 2, waiting)
+                    finish(waiting)
+                    multiply_tile(j, c0 + N_TILE // 2, N_TILE // 2, waiting)
+                else:
+                    multiply_tile(j, c0, N_TILE, waiting)
         for i in range(len(waiting)):
             finish(waiting)

@@ -25,6 +25,7 @@ ROW_TILES = S // P
 W_TILES = DM // P
 N_TILE = 512
 N_HALVES = DM // N_TILE
+W_CHUNKS = 4
 GROUP_TILES = 2
 GROUP_ROWS = GROUP_TILES * P
 ROW_GROUPS = ROW_TILES // GROUP_TILES
@@ -32,7 +33,7 @@ W_V = (1,)
 W_V4 = (1, 3)
 H_B = 2
 W_B = 4
-RUN = 2
+RUN = 4
 ACC_TAGS = ("a", "w", "s", "w")
 LOADS = "h0 h1 w0 h2 w1 h3 w2 w3"
 
@@ -57,7 +58,7 @@ def tile_mlstmblock_pb_kernel(tc, h_attn, gn_w, gn_b, W_out, x, skip_scale, out)
         gn_w_sb = keep.tile([P, PASSES, PACK], BF16)
         gn_b_sb = keep.tile([P, PASSES, PACK], BF16)
         h_raw = [keep.tile([P, ROW_TILES, K_PASS], BF16, name="h_raw%d" % g) for g in range(PASSES)]
-        w_raw = [keep.tile([P, W_TILES, K_PASS], BF16, name="w_raw%d" % g) for g in range(PASSES)]
+        w_raw = [keep.tile([P, W_TILES // 2, 2 * K_PASS], BF16, name="w_raw%d" % c) for c in range(W_CHUNKS)]
         x_sb = keep.tile([P, ROW_TILES, DM], BF16)
         skip_bf = keep.tile([P, 1], BF16)
         first = True
@@ -70,7 +71,9 @@ def tile_mlstmblock_pb_kernel(tc, h_attn, gn_w, gn_b, W_out, x, skip_scale, out)
             elif item[0] == "h":
                 nc.sync.dma_start(out=h_raw[g][:], in_=h_rows[:, :, g * K_PASS : (g + 1) * K_PASS])
             else:
-                nc.sync.dma_start(out=w_raw[g][:], in_=w_rows[:, :, g * K_PASS : (g + 1) * K_PASS])
+                tiles = slice(g % 2 * W_TILES // 2, (g % 2 + 1) * W_TILES // 2)
+                channels = slice(g // 2 * 2 * K_PASS, (g // 2 + 1) * 2 * K_PASS)
+                nc.sync.dma_start(out=w_raw[g][:], in_=w_rows[:, tiles, channels])
             if first:
                 nc.sync.dma_start(out=gn_w_sb[:], in_=gn_w.rearrange("(g p t) -> p g t", p=P, t=PACK))
                 nc.sync.dma_start(out=gn_b_sb[:], in_=gn_b.rearrange("(g p t) -> p g t", p=P, t=PACK))
@@ -87,8 +90,8 @@ def tile_mlstmblock_pb_kernel(tc, h_attn, gn_w, gn_b, W_out, x, skip_scale, out)
 
         h_codes = [keep.tile([P, PASSES * GROUP_ROWS], U32, align_bytes=64, name="h_codes%d" % m) for m in range(ROW_GROUPS)]
         h_scales = [keep.tile([P, PASSES * GROUP_ROWS], U8, align_bytes=64, name="h_scales%d" % m) for m in range(ROW_GROUPS)]
-        w_codes = keep.tile([P, PASSES, DM], U32, align_bytes=64)
-        w_scales = keep.tile([P, PASSES, DM], U8, align_bytes=64)
+        w_codes = [keep.tile([P, PASSES * N_TILE], U32, align_bytes=64, name="w_codes%d" % n) for n in range(N_HALVES)]
+        w_scales = [keep.tile([P, PASSES * N_TILE], U8, align_bytes=64, name="w_scales%d" % n) for n in range(N_HALVES)]
         stats_ps = turned.tile([P, PASSES, 6], F32, tag="s", bufs=1, name="stats_ps")
         part = [keep.tile([P, GROUPS_PER_PASS, 2], F32, name="part%d" % g) for g in range(PASSES)]
         late_part0 = keep.tile([P, GROUPS_PER_PASS, 2], F32)
@@ -219,36 +222,39 @@ def tile_mlstmblock_pb_kernel(tc, h_attn, gn_w, gn_b, W_out, x, skip_scale, out)
                 in_=grouped[:, g0:g1].rearrange("p g s t -> p (g s t)"),
             )
 
-        def transpose_w(g, a):
+        def transpose_w(c, a):
             bank = turned.tile([P, 2, 2, P], F32, tag="w", bufs=W_B, name="wT")
-            for c in range(2):
-                words = w_raw[g][:, 2 * a + c, :].bitcast(F32).rearrange("p (q u) -> p u q", u=2)
+            for i in range(2):
+                channels = w_raw[c][:, 2 * (a % 2) + i, a // 2 * K_PASS : (a // 2 + 1) * K_PASS]
+                words = channels.bitcast(F32).rearrange("p (q u) -> p u q", u=2)
                 for u in range(2):
-                    nc.tensor.transpose(out=bank[:, c, u, :], in_=words[:, u, :], identity=ident_f32[:])
+                    nc.tensor.transpose(out=bank[:, i, u, :], in_=words[:, u, :], identity=ident_f32[:])
             return bank
 
         def copy_w(grouped, bank, a, on_scalar):
-            grouped_words = grouped[:].bitcast(F32).rearrange("p (a c m u) -> p a c m u", a=W_TILES // 2, c=2, u=2)
+            grouped_words = grouped[:].bitcast(F32).rearrange("p (a i m u) -> p a i m u", a=4, i=2, u=2)
             copy = nc.scalar.copy if on_scalar else nc.vector.tensor_copy
-            copy(out=grouped_words[:, a], in_=bank[:].rearrange("p c u m -> p c m u"))
+            copy(out=grouped_words[:, a], in_=bank[:].rearrange("p i u m -> p i m u"))
 
-        def quantise_w(g, grouped):
-            nc.vector.quantize_mx(out=w_codes[:, g, :].bitcast(FP8X4), scales=w_scales[:, g, :], in_=grouped[:])
+        def quantise_w(c, grouped):
+            n, words = c % 2, slice(c // 2 * 2 * N_TILE, (c // 2 + 1) * 2 * N_TILE)
+            nc.vector.quantize_mx(out=w_codes[n][:, words].bitcast(FP8X4), scales=w_scales[n][:, words], in_=grouped[:])
 
-        def multiply(acc, j, cols, g):
+        def multiply(acc, j, n, c0, width, g):
             m, i = j // GROUP_TILES, j % GROUP_TILES
             rows = slice(g * GROUP_ROWS + i * P, g * GROUP_ROWS + (i + 1) * P)
+            words = slice(g * N_TILE + c0, g * N_TILE + c0 + width)
             nc.tensor.matmul_mx(
                 out=acc[:], lhsT=h_codes[m][:, rows].bitcast(FP8X4), lhsT_scale=h_scales[m][:, rows],
-                rhs=w_codes[:, g, cols].bitcast(FP8X4), rhs_scale=w_scales[:, g, cols],
+                rhs=w_codes[n][:, words].bitcast(FP8X4), rhs_scale=w_scales[n][:, words],
                 start=(g == 0), stop=(g == PASSES - 1),
             )
 
-        def multiply_tile(j, c0, width, waiting):
+        def multiply_tile(j, n, c0, width, waiting):
             acc = new_acc(width)
-            cols = slice(c0, c0 + width)
+            cols = slice(n * N_TILE + c0, n * N_TILE + c0 + width)
             for g in range(PASSES):
-                multiply(acc, j, cols, g)
+                multiply(acc, j, n, c0, width, g)
             waiting.append((acc, j, cols, width))
 
         def finish(waiting):
@@ -338,12 +344,12 @@ def tile_mlstmblock_pb_kernel(tc, h_attn, gn_w, gn_b, W_out, x, skip_scale, out)
                     finish(waiting)
                 if m + 1 < ROW_GROUPS:
                     pl1[s] = normalise_all(s, hb1[s])
-                j, c0 = (m - 1) * GROUP_TILES + s // N_HALVES, s % N_HALVES * N_TILE
+                j, n = (m - 1) * GROUP_TILES + s % GROUP_TILES, s // GROUP_TILES
                 if m == ROW_GROUPS and s == PASSES - 1:
-                    multiply_tile(j, c0, N_TILE // 2, waiting)
+                    multiply_tile(j, n, 0, N_TILE // 2, waiting)
                     finish(waiting)
-                    multiply_tile(j, c0 + N_TILE // 2, N_TILE // 2, waiting)
+                    multiply_tile(j, n, N_TILE // 2, N_TILE // 2, waiting)
                 else:
-                    multiply_tile(j, c0, N_TILE, waiting)
+                    multiply_tile(j, n, 0, N_TILE, waiting)
         for i in range(len(waiting)):
             finish(waiting)

@@ -33,7 +33,7 @@ W_V = (1,)
 W_V4 = (1, 3)
 H_B = 2
 W_B = 4
-RUN = 4
+RUN = 2
 ACC_TAGS = ("a", "w", "s", "w")
 LOADS = "h0 h1 w0 h2 w1 h3 w2 w3"
 
@@ -208,8 +208,8 @@ def tile_mlstmblock_pb_kernel(tc, h_attn, gn_w, gn_b, W_out, x, skip_scale, out)
         def regroup(g, planes, grouped, on_scalar):
             copy = nc.scalar.copy if on_scalar else nc.vector.tensor_copy
             copy(
-                out=grouped[:, g].rearrange("p (c i) t -> p c t i", i=4),
-                in_=planes[:].rearrange("p t (c i) -> p c t i", i=4),
+                out=grouped[:, g].rearrange("p (c i) t -> p c t i", i=8),
+                in_=planes[:].rearrange("p t (c i) -> p c t i", i=8),
             )
 
         def new_grouped():

@@ -26,15 +26,17 @@ W_TILES = DM // P
 N_TILE = 512
 N_HALVES = DM // N_TILE
 W_CHUNKS = 4
-GROUP_TILES = 2
-GROUP_ROWS = GROUP_TILES * P
-ROW_GROUPS = ROW_TILES // GROUP_TILES
+ROW_GROUPS = ((0, 1), (2, 3), (4, 5), (6, 7))
+S_RG = ((3, 1), (3, 3))
 W_V = (1,)
 W_V4 = (1, 3)
-H_B = 2
-W_B = 4
-RUN = 2
-ACC_TAGS = ("a", "w", "s", "w")
+RUNS = (0, 4, 2, 4, 4)
+SPLIT = (0, 1)
+AHEAD = True
+ACC_TAGS = ("a", "h0", "h1", "w0")
+LATE_BANKS = ("s", "w1", "w2", "w3")
+H_BANKS = ("a", "h0", "h1", "w0")
+W_BANKS = ("w0", "w1", "w2", "w3")
 LOADS = "h0 h1 w0 h2 w1 h3 w2 w3"
 
 FLOPS = 2 * S * DM * DI
@@ -64,7 +66,7 @@ def tile_mlstmblock_pb_kernel(tc, h_attn, gn_w, gn_b, W_out, x, skip_scale, out)
         first = True
         for item in LOADS.split(" "):
             g = int(item[1])
-            if item == "h0":
+            if item[0] == "h" and g in SPLIT:
                 for i in range(2):
                     rows = slice(i * ROW_TILES // 2, (i + 1) * ROW_TILES // 2)
                     nc.sync.dma_start(out=h_raw[g][:, rows, :], in_=h_rows[:, rows, g * K_PASS : (g + 1) * K_PASS])
@@ -88,15 +90,20 @@ def tile_mlstmblock_pb_kernel(tc, h_attn, gn_w, gn_b, W_out, x, skip_scale, out)
         minus_mean_of = keep.tile([P, P], F32)
         nc.vector.memset(minus_mean_of[:], -1.0 / (S * GROUP))
 
-        h_codes = [keep.tile([P, PASSES * GROUP_ROWS], U32, align_bytes=64, name="h_codes%d" % m) for m in range(ROW_GROUPS)]
-        h_scales = [keep.tile([P, PASSES * GROUP_ROWS], U8, align_bytes=64, name="h_scales%d" % m) for m in range(ROW_GROUPS)]
+        h_codes = []
+        h_scales = []
+        for m, tiles in enumerate(ROW_GROUPS):
+            h_codes.append(keep.tile([P, PASSES * len(tiles) * P], U32, align_bytes=64, name="h_codes%d" % m))
+            h_scales.append(keep.tile([P, PASSES * len(tiles) * P], U8, align_bytes=64, name="h_scales%d" % m))
         w_codes = [keep.tile([P, PASSES * N_TILE], U32, align_bytes=64, name="w_codes%d" % n) for n in range(N_HALVES)]
         w_scales = [keep.tile([P, PASSES * N_TILE], U8, align_bytes=64, name="w_scales%d" % n) for n in range(N_HALVES)]
-        stats_ps = turned.tile([P, PASSES, 6], F32, tag="s", bufs=1, name="stats_ps")
+        stats_ps = turned.tile([P, PASSES, 6], F32, tag="s", name="stats_ps")
         part = [keep.tile([P, GROUPS_PER_PASS, 2], F32, name="part%d" % g) for g in range(PASSES)]
-        late_part0 = keep.tile([P, GROUPS_PER_PASS, 2], F32)
-        nc.vector.memset(late_part0[:], 0.0)
-        parts_of = [[part[0], late_part0]] + [[part[g]] for g in range(1, PASSES)]
+        parts_of = [[part[g]] for g in range(PASSES)]
+        for g in SPLIT:
+            second = keep.tile([P, GROUPS_PER_PASS, 2], F32, name="second%d" % g)
+            nc.vector.memset(second[:], 0.0)
+            parts_of[g].append(second)
         quad = [P, PACK]
         gain = [keep.tile(quad, F32, name="gain%d" % g) for g in range(PASSES)]
         shift = [keep.tile(quad, F32, name="shift%d" % g) for g in range(PASSES)]
@@ -122,26 +129,26 @@ def tile_mlstmblock_pb_kernel(tc, h_attn, gn_w, gn_b, W_out, x, skip_scale, out)
         def keep_sums(g):
             nc.vector.tensor_copy(out=part[g][:, :, 0], in_=stats_ps[:, g, 0:2])
 
-        def squares_on_scalar(g, u):
-            parts = parts_of[g]
-            step = ROW_TILES // len(parts)
-            for i, sums_of in enumerate(parts):
-                scratch = stage.tile([P, ROW_TILES, GROUP], BF16, name="scratch_s")
-                nc.scalar.activation(
-                    out=scratch[:, 0:step, :], in_=h_raw[g][:, i * step : (i + 1) * step, u * GROUP : (u + 1) * GROUP], func=ACT.Square,
-                    accum_out=sums_of[:, u, 1:2],
-                )
+        def squares_on_scalar(g, u, i):
+            step = ROW_TILES // len(parts_of[g])
+            scratch = stage.tile([P, ROW_TILES, GROUP], BF16, name="scratch_s")
+            nc.scalar.activation(
+                out=scratch[:, 0:step, :], in_=h_raw[g][:, i * step : (i + 1) * step, u * GROUP : (u + 1) * GROUP],
+                func=ACT.Square, accum_out=parts_of[g][i][:, u, 1:2],
+            )
 
-        def squares_on_vector(g, u):
-            parts = parts_of[g]
-            step = ROW_TILES // len(parts)
-            for i, sums_of in enumerate(parts):
-                group = h_raw[g][:, i * step : (i + 1) * step, u * GROUP : (u + 1) * GROUP]
-                scratch = stage.tile([P, ROW_TILES, GROUP], BF16, name="scratch_v")
-                nc.vector.scalar_tensor_tensor(
-                    out=scratch[:, 0:step, :], in0=group, scalar=1.0, in1=group, op0=ALU.mult, op1=ALU.mult,
-                    accum_out=sums_of[:, u, 1:2],
-                )
+        def squares_on_vector(g, u, i):
+            step = ROW_TILES // len(parts_of[g])
+            group = h_raw[g][:, i * step : (i + 1) * step, u * GROUP : (u + 1) * GROUP]
+            scratch = stage.tile([P, ROW_TILES, GROUP], BF16, name="scratch_v")
+            nc.vector.scalar_tensor_tensor(
+                out=scratch[:, 0:step, :], in0=group, scalar=1.0, in1=group, op0=ALU.mult, op1=ALU.mult,
+                accum_out=parts_of[g][i][:, u, 1:2],
+            )
+
+        def squares(g, i):
+            squares_on_vector(g, 1, i)
+            squares_on_scalar(g, 0, i)
 
         def totals(g):
             for i, sums_of in enumerate(parts_of[g]):
@@ -176,33 +183,24 @@ def tile_mlstmblock_pb_kernel(tc, h_attn, gn_w, gn_b, W_out, x, skip_scale, out)
 
         def transpose_h(m, g):
             words = h_raw[g][:].rearrange("p j c -> p (j c)").bitcast(F32).rearrange("p (j q u) -> p j u q", j=ROW_TILES, u=2)
-            tag = "a" if m == 1 and g == 0 else ("w" if m > 0 and g % 2 == 1 else "h")
-            bank = turned.tile([P, 2, GROUP_TILES, P], F32, tag=tag, bufs={"w": W_B, "h": H_B}.get(tag, 1), name="hT")
+            tiles = ROW_GROUPS[m]
+            tag = H_BANKS[1 + g % 2] if m == 0 else (H_BANKS[g] if m == 1 else LATE_BANKS[g])
+            bank = turned.tile([P, 2, len(tiles), P], F32, tag=tag, name="hT")
             for u in range(2):
-                for i in range(GROUP_TILES):
-                    nc.tensor.transpose(
-                        out=bank[:, u, i, :], in_=words[:, m * GROUP_TILES + i, u, :], identity=ident_f32[:]
-                    )
+                for i, j in enumerate(tiles):
+                    nc.tensor.transpose(out=bank[:, u, i, :], in_=words[:, j, u, :], identity=ident_f32[:])
             return bank
 
-        def normalise(g, bank, planes, t, on_scalar):
-            u, e = t // 2, t % 2
-            values = bank[:, u].rearrange("p i r -> p (i r)").bitcast(BF16).rearrange("p (r e) -> p e r", e=2)[:, e, :]
-            if on_scalar:
+        def normalise_all(m, g, bank):
+            rows = len(ROW_GROUPS[m]) * P
+            planes = planes_pool.tile([P, PACK, rows], BF16, name="planes")
+            for t in range(PACK):
+                u, e = t // 2, t % 2
+                values = bank[:, u].rearrange("p i r -> p (i r)").bitcast(BF16).rearrange("p (r e) -> p e r", e=2)[:, e, :]
                 nc.scalar.activation(
                     out=planes[:, t, :], in_=values, func=ACT.Identity,
                     scale=gain[g][:, t : t + 1], bias=shift[g][:, t : t + 1],
                 )
-            else:
-                nc.vector.tensor_scalar(
-                    out=planes[:, t, :], in0=values, scalar1=gain[g][:, t : t + 1],
-                    scalar2=shift[g][:, t : t + 1], op0=ALU.mult, op1=ALU.add,
-                )
-
-        def normalise_all(g, bank):
-            planes = planes_pool.tile([P, PACK, GROUP_ROWS], BF16, name="planes")
-            for t in range(PACK):
-                normalise(g, bank, planes, t, True)
             return planes
 
         def regroup(g, planes, grouped, on_scalar):
@@ -212,18 +210,19 @@ def tile_mlstmblock_pb_kernel(tc, h_attn, gn_w, gn_b, W_out, x, skip_scale, out)
                 in_=planes[:].rearrange("p t (c i) -> p c t i", i=8),
             )
 
-        def new_grouped():
-            return stage.tile([P, PASSES, GROUP_ROWS, PACK], BF16, align_bytes=64, name="h_grouped")
+        def new_grouped(m):
+            return stage.tile([P, PASSES, len(ROW_GROUPS[m]) * P, PACK], BF16, align_bytes=64, name="h_grouped")
 
         def quantise_h(m, g0, g1, grouped):
-            cols = slice(g0 * GROUP_ROWS, g1 * GROUP_ROWS)
+            rows = len(ROW_GROUPS[m]) * P
+            cols = slice(g0 * rows, g1 * rows)
             nc.vector.quantize_mx(
                 out=h_codes[m][:, cols].bitcast(FP8X4), scales=h_scales[m][:, cols],
                 in_=grouped[:, g0:g1].rearrange("p g s t -> p (g s t)"),
             )
 
         def transpose_w(c, a):
-            bank = turned.tile([P, 2, 2, P], F32, tag="w", bufs=W_B, name="wT")
+            bank = turned.tile([P, 2, 2, P], F32, tag=W_BANKS[a], name="wT")
             for i in range(2):
                 channels = w_raw[c][:, 2 * (a % 2) + i, a // 2 * K_PASS : (a // 2 + 1) * K_PASS]
                 words = channels.bitcast(F32).rearrange("p (q u) -> p u q", u=2)
@@ -240,9 +239,9 @@ def tile_mlstmblock_pb_kernel(tc, h_attn, gn_w, gn_b, W_out, x, skip_scale, out)
             n, words = c % 2, slice(c // 2 * 2 * N_TILE, (c // 2 + 1) * 2 * N_TILE)
             nc.vector.quantize_mx(out=w_codes[n][:, words].bitcast(FP8X4), scales=w_scales[n][:, words], in_=grouped[:])
 
-        def multiply(acc, j, n, c0, width, g):
-            m, i = j // GROUP_TILES, j % GROUP_TILES
-            rows = slice(g * GROUP_ROWS + i * P, g * GROUP_ROWS + (i + 1) * P)
+        def multiply(acc, m, i, n, c0, width, g):
+            first = (g * len(ROW_GROUPS[m]) + i) * P
+            rows = slice(first, first + P)
             words = slice(g * N_TILE + c0, g * N_TILE + c0 + width)
             nc.tensor.matmul_mx(
                 out=acc[:], lhsT=h_codes[m][:, rows].bitcast(FP8X4), lhsT_scale=h_scales[m][:, rows],
@@ -250,12 +249,12 @@ def tile_mlstmblock_pb_kernel(tc, h_attn, gn_w, gn_b, W_out, x, skip_scale, out)
                 start=(g == 0), stop=(g == PASSES - 1),
             )
 
-        def multiply_tile(j, n, c0, width, waiting):
+        def multiply_tile(m, i, n, c0, width, waiting):
             acc = new_acc(width)
             cols = slice(n * N_TILE + c0, n * N_TILE + c0 + width)
             for g in range(PASSES):
-                multiply(acc, j, n, c0, width, g)
-            waiting.append((acc, j, cols, width))
+                multiply(acc, m, i, n, c0, width, g)
+            waiting.append((acc, ROW_GROUPS[m][i], cols, width))
 
         def finish(waiting):
             acc, j, cols, width = waiting[0]
@@ -277,22 +276,23 @@ def tile_mlstmblock_pb_kernel(tc, h_attn, gn_w, gn_b, W_out, x, skip_scale, out)
         def new_acc(width):
             tag = ACC_TAGS[len(acc_tags) % len(ACC_TAGS)]
             acc_tags.append(tag)
-            return turned.tile([P, width], F32, tag=tag, bufs=W_B if tag == "w" else 1, name="acc")
+            return turned.tile([P, width], F32, tag=tag, name="acc")
 
         hb = {}
         pl = {}
         wg = {}
         hb1 = {}
         pl1 = {}
-        grouped = {0: new_grouped(), 1: new_grouped()}
+        grouped = {0: new_grouped(0), 1: new_grouped(1)}
         for k in range(PASSES + 2):
             now, last, older = k < PASSES, 0 <= k - 1 < PASSES, 0 <= k - 2 < PASSES
             if now:
-                squares_on_vector(k, 1)
+                for i in range(len(parts_of[k])):
+                    if not (AHEAD and k == 1 and i == 0):
+                        squares(k, i)
                 sums(k)
-                squares_on_scalar(k, 0)
             if last:
-                pl[k - 1] = normalise_all(k - 1, hb[k - 1])
+                pl[k - 1] = normalise_all(0, k - 1, hb[k - 1])
             if now:
                 keep_sums(k)
                 hb[k] = transpose_h(0, k)
@@ -302,6 +302,8 @@ def tile_mlstmblock_pb_kernel(tc, h_attn, gn_w, gn_b, W_out, x, skip_scale, out)
                 move_w(k - 1, 1)
             if now:
                 totals(k)
+                if AHEAD and k == 0:
+                    squares(1, 0)
                 keep_moments(k)
             if last:
                 move_w(k - 1, 2)
@@ -323,33 +325,40 @@ def tile_mlstmblock_pb_kernel(tc, h_attn, gn_w, gn_b, W_out, x, skip_scale, out)
                 for g in range(PASSES):
                     if g > 0:
                         hb1[g] = transpose_h(1, g)
-                    pl1[g] = normalise_all(g, hb1[g])
+                    pl1[g] = normalise_all(1, g, hb1[g])
             if k == 2:
                 hb1[0] = transpose_h(1, 0)
         nc.vector.tensor_copy(out=skip[:], in_=skip_bf[:])
 
         waiting = []
-        for m in range(1, ROW_GROUPS + 1):
-            if 1 < m < ROW_GROUPS:
-                grouped[m] = new_grouped()
+        groups = len(ROW_GROUPS)
+        for m in range(1, groups + 1):
+            if 1 < m < groups:
+                grouped[m] = new_grouped(m)
+            tiles = [(m - 1, i, n) for n in range(N_HALVES) for i in range(len(ROW_GROUPS[m - 1]))]
             for s in range(PASSES):
-                if m + 1 < ROW_GROUPS and s % RUN == 0:
-                    for g in range(s, s + RUN):
+                run = RUNS[m]
+                if m + 1 < groups and s % run == 0:
+                    for g in range(s, s + run):
                         hb1[g] = transpose_h(m + 1, g)
-                if m < ROW_GROUPS:
-                    regroup(s, pl1[s], grouped[m], m == ROW_GROUPS - 1 and s % 2 == 1)
+                if m < groups:
+                    regroup(s, pl1[s], grouped[m], (m, s) in S_RG)
                     if s == PASSES - 1:
                         quantise_h(m, 0, PASSES, grouped[m])
-                if len(waiting) > (1 if m < ROW_GROUPS else 0):
+                if len(waiting) > (1 if m < groups else 0):
                     finish(waiting)
-                if m + 1 < ROW_GROUPS:
-                    pl1[s] = normalise_all(s, hb1[s])
-                j, n = (m - 1) * GROUP_TILES + s % GROUP_TILES, s // GROUP_TILES
-                if m == ROW_GROUPS and s == PASSES - 1:
-                    multiply_tile(j, n, 0, N_TILE // 2, waiting)
-                    finish(waiting)
-                    multiply_tile(j, n, N_TILE // 2, N_TILE // 2, waiting)
+                if m + 1 < groups:
+                    pl1[s] = normalise_all(m + 1, s, hb1[s])
+                if len(tiles) == PASSES:
+                    mine = tiles[s : s + 1]
                 else:
-                    multiply_tile(j, n, 0, N_TILE, waiting)
+                    mine = tiles[s // 2 : s // 2 + 1] if s % 2 == 1 else []
+                for m1, i, n in mine:
+                    if m == groups and s == PASSES - 1:
+                        multiply_tile(m1, i, n, 0, N_TILE // 2, waiting)
+                        finish(waiting)
+                        multiply_tile(m1, i, n, N_TILE // 2, N_TILE // 2, waiting)
+                    else:
+                        multiply_tile(m1, i, n, 0, N_TILE, waiting)
         for i in range(len(waiting)):
             finish(waiting)

@@ -28,11 +28,9 @@ N_HALVES = DM // N_TILE
 W_CHUNKS = 4
 ROW_GROUPS = ((0, 1), (2, 3), (4, 5), (6, 7))
 S_RG = ((3, 1), (3, 3))
-W_V = (1,)
-W_V4 = (1, 3)
+SQUARED_ON_TENSOR = (2, 3)
 RUNS = (0, 4, 2, 4, 4)
 SPLIT = (0, 1)
-AHEAD = True
 ACC_TAGS = ("a", "h0", "h1", "w0")
 LATE_BANKS = ("s", "w1", "w2", "w3")
 H_BANKS = ("a", "h0", "h1", "w0")
@@ -146,8 +144,26 @@ def tile_mlstmblock_pb_kernel(tc, h_attn, gn_w, gn_b, W_out, x, skip_scale, out)
                 accum_out=parts_of[g][i][:, u, 1:2],
             )
 
+        def product_of_squares(g):
+            bank = turned.tile([P, P], F32, tag="a", name="gram")
+            for j in range(ROW_TILES):
+                for c in range(2):
+                    chunk = h_raw[g][:, j, GROUP + c * P : GROUP + (c + 1) * P]
+                    nc.tensor.matmul(
+                        out=bank[:], lhsT=chunk, rhs=chunk, start=(j == 0 and c == 0), stop=(j == ROW_TILES - 1 and c == 1)
+                    )
+            return bank
+
+        def diagonal(g, bank):
+            scratch = stage.tile([P, P], F32, name="scratch_d")
+            nc.vector.scalar_tensor_tensor(
+                out=scratch[:], in0=bank[:], scalar=1.0, in1=ident_f32[:], op0=ALU.mult, op1=ALU.mult,
+                accum_out=part[g][:, 1, 1:2],
+            )
+
         def squares(g, i):
-            squares_on_vector(g, 1, i)
+            if g not in SQUARED_ON_TENSOR:
+                squares_on_vector(g, 1, i)
             squares_on_scalar(g, 0, i)
 
         def totals(g):
@@ -271,7 +287,7 @@ def tile_mlstmblock_pb_kernel(tc, h_attn, gn_w, gn_b, W_out, x, skip_scale, out)
             return stage.tile([P, DM * PACK], BF16, align_bytes=64, name="w_grouped")
 
         def move_w(g, a):
-            copy_w(wg[g], transpose_w(g, a), a, a not in (W_V if g < PASSES - 1 else W_V4))
+            copy_w(wg[g], transpose_w(g, a), a, a % 2 == 0)
 
         def new_acc(width):
             tag = ACC_TAGS[len(acc_tags) % len(ACC_TAGS)]
@@ -286,11 +302,17 @@ def tile_mlstmblock_pb_kernel(tc, h_attn, gn_w, gn_b, W_out, x, skip_scale, out)
         grouped = {0: new_grouped(0), 1: new_grouped(1)}
         for k in range(PASSES + 2):
             now, last, older = k < PASSES, 0 <= k - 1 < PASSES, 0 <= k - 2 < PASSES
+            if k in SQUARED_ON_TENSOR:
+                products = product_of_squares(k)
+            if older:
+                quantise_w(k - 2, wg[k - 2])
             if now:
                 for i in range(len(parts_of[k])):
-                    if not (AHEAD and k == 1 and i == 0):
+                    if not (k == 1 and i == 0):
                         squares(k, i)
                 sums(k)
+            if k in SQUARED_ON_TENSOR:
+                diagonal(k, products)
             if last:
                 pl[k - 1] = normalise_all(0, k - 1, hb[k - 1])
             if now:
@@ -302,32 +324,28 @@ def tile_mlstmblock_pb_kernel(tc, h_attn, gn_w, gn_b, W_out, x, skip_scale, out)
                 move_w(k - 1, 1)
             if now:
                 totals(k)
-                if AHEAD and k == 0:
+                if k == 0:
                     squares(1, 0)
                 keep_moments(k)
-            if last:
-                move_w(k - 1, 2)
-            if older:
-                quantise_w(k - 2, wg[k - 2])
-            if now:
                 negative_variance(k)
             if last:
                 regroup(k - 1, pl[k - 1], grouped[0], False)
+                move_w(k - 1, 2)
             if now:
                 gain_of(k)
             if last:
                 move_w(k - 1, 3)
+            if k == PASSES - 1:
+                hb1[0] = transpose_h(1, 0)
             if now:
                 shift_of(k)
-            if last:
-                quantise_h(0, k - 1, k, grouped[0])
             if k == PASSES:
                 for g in range(PASSES):
                     if g > 0:
                         hb1[g] = transpose_h(1, g)
                     pl1[g] = normalise_all(1, g, hb1[g])
-            if k == 2:
-                hb1[0] = transpose_h(1, 0)
+            if last:
+                quantise_h(0, k - 1, k, grouped[0])
         nc.vector.tensor_copy(out=skip[:], in_=skip_bf[:])
 
         waiting = []

@@ -287,7 +287,7 @@ def tile_mlstmblock_pb_kernel(tc, h_attn, gn_w, gn_b, W_out, x, skip_scale, out)
             return stage.tile([P, DM * PACK], BF16, align_bytes=64, name="w_grouped")
 
         def move_w(g, a):
-            copy_w(wg[g], transpose_w(g, a), a, a % 2 == 0)
+            copy_w(wg[g], transpose_w(g, a), a, a % 2 == 1)
 
         def new_acc(width):
             tag = ACC_TAGS[len(acc_tags) % len(ACC_TAGS)]
@@ -344,8 +344,8 @@ def tile_mlstmblock_pb_kernel(tc, h_attn, gn_w, gn_b, W_out, x, skip_scale, out)
                     if g > 0:
                         hb1[g] = transpose_h(1, g)
                     pl1[g] = normalise_all(1, g, hb1[g])
-            if last:
-                quantise_h(0, k - 1, k, grouped[0])
+            if last and k % 2 == 0:
+                quantise_h(0, k - 2, k, grouped[0])
         nc.vector.tensor_copy(out=skip[:], in_=skip_bf[:])
 
         waiting = []

@@ -28,9 +28,13 @@ N_HALVES = DM // N_TILE
 W_CHUNKS = 4
 ROW_GROUPS = ((0, 1), (2, 3), (4, 5), (6, 7))
 S_RG = ((3, 1), (3, 3))
-SQUARED_ON_TENSOR = (2, 3)
+ON_TENSOR = ((1, 1), (2, 1), (3, 1))
 RUNS = (0, 4, 2, 4, 4)
-SPLIT = (0, 1)
+PIECES = {0: (4, 4), 1: (8,), 2: (8,), 3: (8,)}
+PAD = 8
+PITCH = PAD + K_PASS
+SIDE = 132
+STATS_BANKS = ("a", "s")
 ACC_TAGS = ("a", "h0", "h1", "w0")
 LATE_BANKS = ("s", "w1", "w2", "w3")
 H_BANKS = ("a", "h0", "h1", "w0")
@@ -57,19 +61,19 @@ def tile_mlstmblock_pb_kernel(tc, h_attn, gn_w, gn_b, W_out, x, skip_scale, out)
 
         gn_w_sb = keep.tile([P, PASSES, PACK], BF16)
         gn_b_sb = keep.tile([P, PASSES, PACK], BF16)
-        h_raw = [keep.tile([P, ROW_TILES, K_PASS], BF16, name="h_raw%d" % g) for g in range(PASSES)]
+        h_raw = [keep.tile([P, ROW_TILES + 1, PITCH], BF16, name="h_raw%d" % g) for g in range(PASSES)]
+        for g, u in ON_TENSOR:
+            nc.vector.memset(h_raw[g][:, :, 0:PAD], 1.0)
         w_raw = [keep.tile([P, W_TILES // 2, 2 * K_PASS], BF16, name="w_raw%d" % c) for c in range(W_CHUNKS)]
         x_sb = keep.tile([P, ROW_TILES, DM], BF16)
         skip_bf = keep.tile([P, 1], BF16)
         first = True
         for item in LOADS.split(" "):
             g = int(item[1])
-            if item[0] == "h" and g in SPLIT:
-                for i in range(2):
-                    rows = slice(i * ROW_TILES // 2, (i + 1) * ROW_TILES // 2)
-                    nc.sync.dma_start(out=h_raw[g][:, rows, :], in_=h_rows[:, rows, g * K_PASS : (g + 1) * K_PASS])
-            elif item[0] == "h":
-                nc.sync.dma_start(out=h_raw[g][:], in_=h_rows[:, :, g * K_PASS : (g + 1) * K_PASS])
+            if item[0] == "h":
+                for i in range(len(PIECES[g])):
+                    rows = slice(sum(PIECES[g][:i]), sum(PIECES[g][: i + 1]))
+                    nc.sync.dma_start(out=h_raw[g][:, rows, PAD:PITCH], in_=h_rows[:, rows, g * K_PASS : (g + 1) * K_PASS])
             else:
                 tiles = slice(g % 2 * W_TILES // 2, (g % 2 + 1) * W_TILES // 2)
                 channels = slice(g // 2 * 2 * K_PASS, (g // 2 + 1) * 2 * K_PASS)
@@ -95,13 +99,14 @@ def tile_mlstmblock_pb_kernel(tc, h_attn, gn_w, gn_b, W_out, x, skip_scale, out)
             h_scales.append(keep.tile([P, PASSES * len(tiles) * P], U8, align_bytes=64, name="h_scales%d" % m))
         w_codes = [keep.tile([P, PASSES * N_TILE], U32, align_bytes=64, name="w_codes%d" % n) for n in range(N_HALVES)]
         w_scales = [keep.tile([P, PASSES * N_TILE], U8, align_bytes=64, name="w_scales%d" % n) for n in range(N_HALVES)]
-        stats_ps = turned.tile([P, PASSES, 6], F32, tag="s", name="stats_ps")
+        stats_ps = {}
         part = [keep.tile([P, GROUPS_PER_PASS, 2], F32, name="part%d" % g) for g in range(PASSES)]
         parts_of = [[part[g]] for g in range(PASSES)]
-        for g in SPLIT:
-            second = keep.tile([P, GROUPS_PER_PASS, 2], F32, name="second%d" % g)
-            nc.vector.memset(second[:], 0.0)
-            parts_of[g].append(second)
+        for g in range(PASSES):
+            for i in range(1, len(PIECES[g])):
+                more = keep.tile([P, GROUPS_PER_PASS, 2], F32, name="more%d_%d" % (g, i))
+                nc.vector.memset(more[:], 0.0)
+                parts_of[g].append(more)
         quad = [P, PACK]
         gain = [keep.tile(quad, F32, name="gain%d" % g) for g in range(PASSES)]
         shift = [keep.tile(quad, F32, name="shift%d" % g) for g in range(PASSES)]
@@ -114,72 +119,80 @@ def tile_mlstmblock_pb_kernel(tc, h_attn, gn_w, gn_b, W_out, x, skip_scale, out)
         rstd = [keep.tile([P, 1], F32, name="rstd%d" % g) for g in range(PASSES)]
         nc.scalar.activation(out=rstd[0][:], in_=eps[:], func=ACT.Abs_reciprocal_sqrt)
 
+        def new_stats(g):
+            stats_ps[g] = turned.tile([P, 2 * SIDE + 4], F32, tag=STATS_BANKS[g % 2], name="stats_ps")
+
         def sums(g):
             for u in range(GROUPS_PER_PASS):
+                if (g, u) in ON_TENSOR:
+                    continue
                 for j in range(ROW_TILES):
                     for c in range(2):
-                        at = u * GROUP + c * P
+                        at = PAD + u * GROUP + c * P
                         nc.tensor.matmul(
-                            out=stats_ps[:, g, u : u + 1], lhsT=h_raw[g][:, j, at : at + P], rhs=ones[:],
+                            out=stats_ps[g][:, u * (2 * SIDE - 3) : u * (2 * SIDE - 3) + 1],
+                            lhsT=h_raw[g][:, j, at : at + P], rhs=ones[:],
                             start=(j == 0 and c == 0), stop=(j == ROW_TILES - 1 and c == 1),
                         )
 
         def keep_sums(g):
-            nc.vector.tensor_copy(out=part[g][:, :, 0], in_=stats_ps[:, g, 0:2])
+            nc.vector.tensor_copy(out=part[g][:, :, 0], in_=stats_ps[g][:, 0 : 2 * SIDE - 2 : 2 * SIDE - 3])
 
         def squares_on_scalar(g, u, i):
-            step = ROW_TILES // len(parts_of[g])
+            rows = slice(sum(PIECES[g][:i]), sum(PIECES[g][: i + 1]))
             scratch = stage.tile([P, ROW_TILES, GROUP], BF16, name="scratch_s")
             nc.scalar.activation(
-                out=scratch[:, 0:step, :], in_=h_raw[g][:, i * step : (i + 1) * step, u * GROUP : (u + 1) * GROUP],
+                out=scratch[:, 0 : PIECES[g][i], :], in_=h_raw[g][:, rows, PAD + u * GROUP : PAD + (u + 1) * GROUP],
                 func=ACT.Square, accum_out=parts_of[g][i][:, u, 1:2],
             )
 
         def squares_on_vector(g, u, i):
-            step = ROW_TILES // len(parts_of[g])
-            group = h_raw[g][:, i * step : (i + 1) * step, u * GROUP : (u + 1) * GROUP]
+            rows = slice(sum(PIECES[g][:i]), sum(PIECES[g][: i + 1]))
+            group = h_raw[g][:, rows, PAD + u * GROUP : PAD + (u + 1) * GROUP]
             scratch = stage.tile([P, ROW_TILES, GROUP], BF16, name="scratch_v")
             nc.vector.scalar_tensor_tensor(
-                out=scratch[:, 0:step, :], in0=group, scalar=1.0, in1=group, op0=ALU.mult, op1=ALU.mult,
+                out=scratch[:, 0 : PIECES[g][i], :], in0=group, scalar=1.0, in1=group, op0=ALU.mult, op1=ALU.mult,
                 accum_out=parts_of[g][i][:, u, 1:2],
             )
 
-        def product_of_squares(g):
-            bank = turned.tile([P, P], F32, tag="a", name="gram")
+        def products(g, u):
+            flat = h_raw[g][:].rearrange("p j c -> p (j c)")
             for j in range(ROW_TILES):
-                for c in range(2):
-                    chunk = h_raw[g][:, j, GROUP + c * P : GROUP + (c + 1) * P]
+                for e in range(2):
+                    at = j * PITCH + PAD + u * GROUP + e
+                    moving = at - 2 if u == 0 else at
                     nc.tensor.matmul(
-                        out=bank[:], lhsT=chunk, rhs=chunk, start=(j == 0 and c == 0), stop=(j == ROW_TILES - 1 and c == 1)
+                        out=stats_ps[g][:, u * (SIDE + 1) : u * (SIDE + 1) + P + 1],
+                        lhsT=flat[:, at : at + GROUP - 1 : 2], rhs=flat[:, moving : moving + GROUP + 1 : 2],
+                        start=(j == 0 and e == 0), stop=(j == ROW_TILES - 1 and e == 1),
                     )
-            return bank
 
-        def diagonal(g, bank):
+        def diagonal(g, u):
             scratch = stage.tile([P, P], F32, name="scratch_d")
             nc.vector.scalar_tensor_tensor(
-                out=scratch[:], in0=bank[:], scalar=1.0, in1=ident_f32[:], op0=ALU.mult, op1=ALU.mult,
-                accum_out=part[g][:, 1, 1:2],
+                out=scratch[:], in0=stats_ps[g][:, u * SIDE + 1 : u * SIDE + 1 + P], scalar=1.0, in1=ident_f32[:],
+                op0=ALU.mult, op1=ALU.mult, accum_out=part[g][:, u, 1:2],
             )
 
         def squares(g, i):
-            if g not in SQUARED_ON_TENSOR:
+            if (g, 1) not in ON_TENSOR:
                 squares_on_vector(g, 1, i)
             squares_on_scalar(g, 0, i)
 
         def totals(g):
             for i, sums_of in enumerate(parts_of[g]):
                 nc.tensor.matmul(
-                    out=stats_ps[:, g, 2:6], lhsT=minus_mean_of[:], rhs=sums_of[:].rearrange("p u k -> p (u k)"),
+                    out=stats_ps[g][:, 2 * SIDE : 2 * SIDE + 4], lhsT=minus_mean_of[:],
+                    rhs=sums_of[:].rearrange("p u k -> p (u k)"),
                     start=(i == 0), stop=(i == len(parts_of[g]) - 1),
                 )
 
-        def keep_moments(g):
+        def square_of_mean(g):
             half = P // GROUPS_PER_PASS
             for u in range(GROUPS_PER_PASS):
                 channels = slice(u * half, (u + 1) * half)
-                nc.vector.tensor_copy(out=moments[g][channels, :], in_=stats_ps[channels, g, 2 + 2 * u : 4 + 2 * u])
-
-        def negative_variance(g):
+                at = 2 * SIDE + 2 * u
+                nc.vector.tensor_copy(out=moments[g][channels, :], in_=stats_ps[g][channels, at : at + 2])
             nc.vector.scalar_tensor_tensor(
                 out=negvar[g][:], in0=moments[g][:, 0:1], scalar=moments[g][:, 0:1], in1=moments[g][:, 1:2],
                 op0=ALU.mult, op1=ALU.add,
@@ -198,13 +211,13 @@ def tile_mlstmblock_pb_kernel(tc, h_attn, gn_w, gn_b, W_out, x, skip_scale, out)
             )
 
         def transpose_h(m, g):
-            words = h_raw[g][:].rearrange("p j c -> p (j c)").bitcast(F32).rearrange("p (j q u) -> p j u q", j=ROW_TILES, u=2)
+            words = h_raw[g][:].rearrange("p j c -> p (j c)").bitcast(F32).rearrange("p (j w) -> p j w", j=ROW_TILES + 1)
             tiles = ROW_GROUPS[m]
             tag = H_BANKS[1 + g % 2] if m == 0 else (H_BANKS[g] if m == 1 else LATE_BANKS[g])
             bank = turned.tile([P, 2, len(tiles), P], F32, tag=tag, name="hT")
             for u in range(2):
                 for i, j in enumerate(tiles):
-                    nc.tensor.transpose(out=bank[:, u, i, :], in_=words[:, j, u, :], identity=ident_f32[:])
+                    nc.tensor.transpose(out=bank[:, u, i, :], in_=words[:, j, PAD // 2 + u : PITCH // 2 : 2], identity=ident_f32[:])
             return bank
 
         def normalise_all(m, g, bank):
@@ -302,17 +315,18 @@ def tile_mlstmblock_pb_kernel(tc, h_attn, gn_w, gn_b, W_out, x, skip_scale, out)
         grouped = {0: new_grouped(0), 1: new_grouped(1)}
         for k in range(PASSES + 2):
             now, last, older = k < PASSES, 0 <= k - 1 < PASSES, 0 <= k - 2 < PASSES
-            if k in SQUARED_ON_TENSOR:
-                products = product_of_squares(k)
+            if now:
+                new_stats(k)
+                if (k, 1) in ON_TENSOR:
+                    products(k, 1)
             if older:
                 quantise_w(k - 2, wg[k - 2])
             if now:
-                for i in range(len(parts_of[k])):
-                    if not (k == 1 and i == 0):
-                        squares(k, i)
+                for i in range(len(PIECES[k])):
+                    squares(k, i)
                 sums(k)
-            if k in SQUARED_ON_TENSOR:
-                diagonal(k, products)
+                if (k, 1) in ON_TENSOR:
+                    diagonal(k, 1)
             if last:
                 pl[k - 1] = normalise_all(0, k - 1, hb[k - 1])
             if now:
@@ -324,10 +338,7 @@ def tile_mlstmblock_pb_kernel(tc, h_attn, gn_w, gn_b, W_out, x, skip_scale, out)
                 move_w(k - 1, 1)
             if now:
                 totals(k)
-                if k == 0:
-                    squares(1, 0)
-                keep_moments(k)
-                negative_variance(k)
+                square_of_mean(k)
             if last:
                 regroup(k - 1, pl[k - 1], grouped[0], False)
                 move_w(k - 1, 2)

@@ -28,9 +28,9 @@ N_HALVES = DM // N_TILE
 W_CHUNKS = 4
 ROW_GROUPS = ((0, 1), (2, 3), (4, 5), (6, 7))
 S_RG = ((3, 1), (3, 3))
-ON_TENSOR = ((1, 1), (2, 1), (3, 1))
+ON_TENSOR = ((2, 1), (3, 1))
 RUNS = (0, 4, 2, 4, 4)
-PIECES = {0: (4, 4), 1: (8,), 2: (8,), 3: (8,)}
+PIECES = {0: (4, 4), 1: (4, 4), 2: (8,), 3: (8,)}
 PAD = 8
 PITCH = PAD + K_PASS
 SIDE = 132
@@ -38,6 +38,8 @@ STATS_BANKS = ("a", "s")
 ACC_TAGS = ("a", "h0", "h1", "w0")
 LATE_BANKS = ("s", "w1", "w2", "w3")
 H_BANKS = ("a", "h0", "h1", "w0")
+W_PIECES = 2
+W_ORDER = (0, 2, 1, 3)
 W_BANKS = ("w0", "w1", "w2", "w3")
 LOADS = "h0 h1 w0 h2 w1 h3 w2 w3"
 
@@ -77,7 +79,10 @@ def tile_mlstmblock_pb_kernel(tc, h_attn, gn_w, gn_b, W_out, x, skip_scale, out)
             else:
                 tiles = slice(g % 2 * W_TILES // 2, (g % 2 + 1) * W_TILES // 2)
                 channels = slice(g // 2 * 2 * K_PASS, (g // 2 + 1) * 2 * K_PASS)
-                nc.sync.dma_start(out=w_raw[g][:], in_=w_rows[:, tiles, channels])
+                for i in range(W_PIECES):
+                    n = W_TILES // 2 // W_PIECES
+                    piece = slice(i * n, (i + 1) * n)
+                    nc.sync.dma_start(out=w_raw[g][:, piece], in_=w_rows[:, tiles, channels][:, piece])
             if first:
                 nc.sync.dma_start(out=gn_w_sb[:], in_=gn_w.rearrange("(g p t) -> p g t", p=P, t=PACK))
                 nc.sync.dma_start(out=gn_b_sb[:], in_=gn_b.rearrange("(g p t) -> p g t", p=P, t=PACK))
@@ -300,7 +305,7 @@ def tile_mlstmblock_pb_kernel(tc, h_attn, gn_w, gn_b, W_out, x, skip_scale, out)
             return stage.tile([P, DM * PACK], BF16, align_bytes=64, name="w_grouped")
 
         def move_w(g, a):
-            copy_w(wg[g], transpose_w(g, a), a, a % 2 == 1)
+            copy_w(wg[g], transpose_w(g, a), a, W_ORDER.index(a) % 2 == 1)
 
         def new_acc(width):
             tag = ACC_TAGS[len(acc_tags) % len(ACC_TAGS)]
@@ -323,7 +328,8 @@ def tile_mlstmblock_pb_kernel(tc, h_attn, gn_w, gn_b, W_out, x, skip_scale, out)
                 quantise_w(k - 2, wg[k - 2])
             if now:
                 for i in range(len(PIECES[k])):
-                    squares(k, i)
+                    if not (k == 1 and i == 0):
+                        squares(k, i)
                 sums(k)
                 if (k, 1) in ON_TENSOR:
                     diagonal(k, 1)
@@ -334,18 +340,20 @@ def tile_mlstmblock_pb_kernel(tc, h_attn, gn_w, gn_b, W_out, x, skip_scale, out)
                 hb[k] = transpose_h(0, k)
             if last:
                 wg[k - 1] = new_w_grouped()
-                move_w(k - 1, 0)
-                move_w(k - 1, 1)
+                move_w(k - 1, W_ORDER[0])
+                move_w(k - 1, W_ORDER[1])
             if now:
                 totals(k)
+                if k == 0:
+                    squares(1, 0)
                 square_of_mean(k)
             if last:
                 regroup(k - 1, pl[k - 1], grouped[0], False)
-                move_w(k - 1, 2)
+                move_w(k - 1, W_ORDER[2])
             if now:
                 gain_of(k)
             if last:
-                move_w(k - 1, 3)
+                move_w(k - 1, W_ORDER[3])
             if k == PASSES - 1:
                 hb1[0] = transpose_h(1, 0)
             if now:

@@ -61,15 +61,15 @@ def tile_mlstmblock_pb_kernel(tc, h_attn, gn_w, gn_b, W_out, x, skip_scale, out)
         planes_pool = ctx.enter_context(tc.tile_pool(name="planes_pool", bufs=6))
         turned = ctx.enter_context(tc.psum_pool(name="turned", bufs=1))
 
-        gn_w_sb = keep.tile([P, PASSES, PACK], BF16)
-        gn_b_sb = keep.tile([P, PASSES, PACK], BF16)
+        gn_rows = keep.tile([P, DI], BF16)
+        nc.vector.memset(gn_rows[:], 0.0)
+        gn_sb = keep.tile([P, PASSES, PACK, 2], F32)
         h_raw = [keep.tile([P, ROW_TILES + 1, PITCH], BF16, name="h_raw%d" % g) for g in range(PASSES)]
         for g, u in ON_TENSOR:
             nc.vector.memset(h_raw[g][:, :, 0:PAD], 1.0)
         w_raw = [keep.tile([P, W_TILES // 2, 2 * K_PASS], BF16, name="w_raw%d" % c) for c in range(W_CHUNKS)]
         x_sb = keep.tile([P, ROW_TILES, DM], BF16)
         skip_bf = keep.tile([P, 1], BF16)
-        first = True
         for item in LOADS.split(" "):
             g = int(item[1])
             if item[0] == "h":
@@ -83,10 +83,8 @@ def tile_mlstmblock_pb_kernel(tc, h_attn, gn_w, gn_b, W_out, x, skip_scale, out)
                     n = W_TILES // 2 // W_PIECES
                     piece = slice(i * n, (i + 1) * n)
                     nc.sync.dma_start(out=w_raw[g][:, piece], in_=w_rows[:, tiles, channels][:, piece])
-            if first:
-                nc.sync.dma_start(out=gn_w_sb[:], in_=gn_w.rearrange("(g p t) -> p g t", p=P, t=PACK))
-                nc.sync.dma_start(out=gn_b_sb[:], in_=gn_b.rearrange("(g p t) -> p g t", p=P, t=PACK))
-                first = False
+        nc.scalar.dma_start(out=gn_rows[0:1, :], in_=gn_w.unsqueeze(0))
+        nc.scalar.dma_start(out=gn_rows[1:2, :], in_=gn_b.unsqueeze(0))
         nc.sync.dma_start(out=x_sb[:], in_=x_rows)
         nc.sync.dma_start(out=skip_bf[:], in_=skip_scale.partition_broadcast(P))
 
@@ -94,6 +92,8 @@ def tile_mlstmblock_pb_kernel(tc, h_attn, gn_w, gn_b, W_out, x, skip_scale, out)
         make_identity(nc, ident_f32[:])
         ones = keep.tile([P, 1], BF16)
         nc.vector.memset(ones[:], 1.0)
+        first_two = keep.tile([P, 2], BF16)
+        nc.vector.tensor_copy(out=first_two[:], in_=ident_f32[:, 0:2])
         minus_mean_of = keep.tile([P, P], F32)
         nc.vector.memset(minus_mean_of[:], -1.0 / (S * GROUP))
 
@@ -123,6 +123,14 @@ def tile_mlstmblock_pb_kernel(tc, h_attn, gn_w, gn_b, W_out, x, skip_scale, out)
         nc.vector.tensor_scalar(out=eps[:], in0=eps[:], scalar1=EPS_GN, scalar2=None, op0=ALU.add)
         rstd = [keep.tile([P, 1], F32, name="rstd%d" % g) for g in range(PASSES)]
         nc.scalar.activation(out=rstd[0][:], in_=eps[:], func=ACT.Abs_reciprocal_sqrt)
+
+        def spread_gn():
+            bank = turned.tile([P, PASSES, PACK, 2], F32, tag="w3", name="gn_ps")
+            for g in range(PASSES):
+                for t in range(PACK):
+                    channels = gn_rows[:, g * K_PASS + t : (g + 1) * K_PASS - PACK + t + 1 : PACK]
+                    nc.tensor.matmul(out=bank[:, g, t, :], lhsT=channels, rhs=first_two[:], start=True, stop=True)
+            nc.vector.tensor_copy(out=gn_sb[:], in_=bank[:])
 
         def new_stats(g):
             stats_ps[g] = turned.tile([P, 2 * SIDE + 4], F32, tag=STATS_BANKS[g % 2], name="stats_ps")
@@ -207,11 +215,11 @@ def tile_mlstmblock_pb_kernel(tc, h_attn, gn_w, gn_b, W_out, x, skip_scale, out)
             nc.scalar.activation(
                 out=rstd[g][:], in_=negvar[g][:], func=ACT.Abs_reciprocal_sqrt, scale=-1.0, bias=eps[:]
             )
-            nc.scalar.activation(out=gain[g][:], in_=gn_w_sb[:, g, :], func=ACT.Identity, scale=rstd[g][:, 0:1])
+            nc.scalar.activation(out=gain[g][:], in_=gn_sb[:, g, :, 0], func=ACT.Identity, scale=rstd[g][:, 0:1])
 
         def shift_of(g):
             nc.vector.scalar_tensor_tensor(
-                out=shift[g][:], in0=gain[g][:], scalar=moments[g][:, 0:1], in1=gn_b_sb[:, g, :],
+                out=shift[g][:], in0=gain[g][:], scalar=moments[g][:, 0:1], in1=gn_sb[:, g, :, 1],
                 op0=ALU.mult, op1=ALU.add,
             )
 
@@ -338,6 +346,8 @@ def tile_mlstmblock_pb_kernel(tc, h_attn, gn_w, gn_b, W_out, x, skip_scale, out)
             if now:
                 keep_sums(k)
                 hb[k] = transpose_h(0, k)
+            if k == 0:
+                spread_gn()
             if last:
                 wg[k - 1] = new_w_grouped()
                 move_w(k - 1, W_ORDER[0])

@@ -70,6 +70,8 @@ def tile_mlstmblock_pb_kernel(tc, h_attn, gn_w, gn_b, W_out, x, skip_scale, out)
         w_raw = [keep.tile([P, W_TILES // 2, 2 * K_PASS], BF16, name="w_raw%d" % c) for c in range(W_CHUNKS)]
         x_sb = keep.tile([P, ROW_TILES, DM], BF16)
         skip_bf = keep.tile([P, 1], BF16)
+        nc.scalar.dma_start(out=gn_rows[0:1, :], in_=gn_w.unsqueeze(0))
+        nc.scalar.dma_start(out=gn_rows[1:2, :], in_=gn_b.unsqueeze(0))
         for item in LOADS.split(" "):
             g = int(item[1])
             if item[0] == "h":
@@ -83,8 +85,6 @@ def tile_mlstmblock_pb_kernel(tc, h_attn, gn_w, gn_b, W_out, x, skip_scale, out)
                     n = W_TILES // 2 // W_PIECES
                     piece = slice(i * n, (i + 1) * n)
                     nc.sync.dma_start(out=w_raw[g][:, piece], in_=w_rows[:, tiles, channels][:, piece])
-        nc.scalar.dma_start(out=gn_rows[0:1, :], in_=gn_w.unsqueeze(0))
-        nc.scalar.dma_start(out=gn_rows[1:2, :], in_=gn_b.unsqueeze(0))
         nc.sync.dma_start(out=x_sb[:], in_=x_rows)
         nc.sync.dma_start(out=skip_bf[:], in_=skip_scale.partition_broadcast(P))
 

@@ -130,7 +130,7 @@ def tile_mlstmblock_pb_kernel(tc, h_attn, gn_w, gn_b, W_out, x, skip_scale, out)
                 for t in range(PACK):
                     channels = gn_rows[:, g * K_PASS + t : (g + 1) * K_PASS - PACK + t + 1 : PACK]
                     nc.tensor.matmul(out=bank[:, g, t, :], lhsT=channels, rhs=first_two[:], start=True, stop=True)
-            nc.vector.tensor_copy(out=gn_sb[:], in_=bank[:])
+            return bank
 
         def new_stats(g):
             stats_ps[g] = turned.tile([P, 2 * SIDE + 4], F32, tag=STATS_BANKS[g % 2], name="stats_ps")
@@ -347,7 +347,7 @@ def tile_mlstmblock_pb_kernel(tc, h_attn, gn_w, gn_b, W_out, x, skip_scale, out)
                 keep_sums(k)
                 hb[k] = transpose_h(0, k)
             if k == 0:
-                spread_gn()
+                gn_bank = spread_gn()
             if last:
                 wg[k - 1] = new_w_grouped()
                 move_w(k - 1, W_ORDER[0])
@@ -357,6 +357,8 @@ def tile_mlstmblock_pb_kernel(tc, h_attn, gn_w, gn_b, W_out, x, skip_scale, out)
                 if k == 0:
                     squares(1, 0)
                 square_of_mean(k)
+            if k == 0:
+                nc.vector.tensor_copy(out=gn_sb[:], in_=gn_bank[:])
             if last:
                 regroup(k - 1, pl[k - 1], grouped[0], False)
                 move_w(k - 1, W_ORDER[2])
@@ -404,7 +406,9 @@ def tile_mlstmblock_pb_kernel(tc, h_attn, gn_w, gn_b, W_out, x, skip_scale, out)
                     if m == groups and s == PASSES - 1:
                         multiply_tile(m1, i, n, 0, N_TILE // 2, waiting)
                         finish(waiting)
-                        multiply_tile(m1, i, n, N_TILE // 2, N_TILE // 2, waiting)
+                        multiply_tile(m1, i, n, N_TILE // 2, N_TILE // 4, waiting)
+                        finish(waiting)
+                        multiply_tile(m1, i, n, 3 * N_TILE // 4, N_TILE // 4, waiting)
                     else:
                         multiply_tile(m1, i, n, 0, N_TILE, waiting)
         for i in range(len(waiting)):

from contextlib import ExitStack

import concourse.mybir as mybir
from concourse.masks import make_identity

F32 = mybir.dt.float32
BF16 = mybir.dt.bfloat16
U32 = mybir.dt.uint32
U8 = mybir.dt.uint8
FP8X4 = mybir.dt.float8_e4m3fn_x4
ALU = mybir.AluOpType
ACT = mybir.ActivationFunctionType

P = 128
PACK = 4
K_PASS = P * PACK
S = 1024
DI = 2048
DM = 1024
GROUP = 256
EPS_GN = 1e-5
PASSES = DI // K_PASS
GROUPS_PER_PASS = K_PASS // GROUP
ROW_TILES = S // P
W_TILES = DM // P
N_TILE = 512
N_HALVES = DM // N_TILE
W_CHUNKS = 4
ROW_GROUPS = ((0, 1), (2, 3), (4, 5), (6, 7))
S_RG = ((3, 1), (3, 3))
ON_TENSOR = ((2, 1), (3, 1))
RUNS = (0, 4, 2, 4, 4)
PIECES = {0: (4, 4), 1: (4, 4), 2: (8,), 3: (8,)}
PAD = 8
PITCH = PAD + K_PASS
SIDE = 132
STATS_BANKS = ("a", "s")
ACC_TAGS = ("a", "h0", "h1", "w0")
LATE_BANKS = ("s", "w1", "w2", "w3")
H_BANKS = ("a", "h0", "h1", "w0")
W_PIECES = 2
W_ORDER = (0, 2, 1, 3)
W_BANKS = ("w0", "w1", "w2", "w3")
LOADS = "h0 h1 w0 h2 w1 h3 w2 w3"

FLOPS = 2 * S * DM * DI


def tile_mlstmblock_pb_kernel(tc, h_attn, gn_w, gn_b, W_out, x, skip_scale, out):
    nc = tc.nc
    h_rows = h_attn.flatten_outer_dims().rearrange("(p j) c -> p j c", j=ROW_TILES)
    x_rows = x.flatten_outer_dims().rearrange("(p j) m -> p j m", j=ROW_TILES)
    out_rows = out.flatten_outer_dims().rearrange("(p j) m -> p j m", j=ROW_TILES)
    w_rows = W_out.rearrange("(t p) c -> p t c", p=P)

    with ExitStack() as ctx:
        ctx.enter_context(tc.manual_schedule())
        keep = ctx.enter_context(tc.tile_pool(name="keep", bufs=1))
        stage = ctx.enter_context(tc.tile_pool(name="stage", bufs=3))
        results = ctx.enter_context(tc.tile_pool(name="results", bufs=8))
        planes_pool = ctx.enter_context(tc.tile_pool(name="planes_pool", bufs=6))
        turned = ctx.enter_context(tc.psum_pool(name="turned", bufs=1))

        gn_rows = keep.tile([P, DI], BF16)
        nc.vector.memset(gn_rows[:], 0.0)
        gn_sb = keep.tile([P, PASSES, PACK, 2], F32)
        h_raw = [keep.tile([P, ROW_TILES + 1, PITCH], BF16, name="h_raw%d" % g) for g in range(PASSES)]
        for g, u in ON_TENSOR:
            nc.vector.memset(h_raw[g][:, :, 0:PAD], 1.0)
        w_raw = [keep.tile([P, W_TILES // 2, 2 * K_PASS], BF16, name="w_raw%d" % c) for c in range(W_CHUNKS)]
        x_sb = keep.tile([P, ROW_TILES, DM], BF16)
        skip_bf = keep.tile([P, 1], BF16)
        nc.scalar.dma_start(out=gn_rows[0:1, :], in_=gn_w.unsqueeze(0))
        nc.scalar.dma_start(out=gn_rows[1:2, :], in_=gn_b.unsqueeze(0))
        for item in LOADS.split(" "):
            g = int(item[1])
            if item[0] == "h":
                for i in range(len(PIECES[g])):
                    rows = slice(sum(PIECES[g][:i]), sum(PIECES[g][: i + 1]))
                    nc.sync.dma_start(out=h_raw[g][:, rows, PAD:PITCH], in_=h_rows[:, rows, g * K_PASS : (g + 1) * K_PASS])
            else:
                tiles = slice(g % 2 * W_TILES // 2, (g % 2 + 1) * W_TILES // 2)
                channels = slice(g // 2 * 2 * K_PASS, (g // 2 + 1) * 2 * K_PASS)
                for i in range(W_PIECES):
                    n = W_TILES // 2 // W_PIECES
                    piece = slice(i * n, (i + 1) * n)
                    nc.sync.dma_start(out=w_raw[g][:, piece], in_=w_rows[:, tiles, channels][:, piece])
        nc.sync.dma_start(out=x_sb[:], in_=x_rows)
        nc.sync.dma_start(out=skip_bf[:], in_=skip_scale.partition_broadcast(P))

        ident_f32 = keep.tile([P, P], F32)
        make_identity(nc, ident_f32[:])
        ones = keep.tile([P, 1], BF16)
        nc.vector.memset(ones[:], 1.0)
        first_two = keep.tile([P, 2], BF16)
        nc.vector.tensor_copy(out=first_two[:], in_=ident_f32[:, 0:2])
        minus_mean_of = keep.tile([P, P], F32)
        nc.vector.memset(minus_mean_of[:], -1.0 / (S * GROUP))

        h_codes = []
        h_scales = []
        for m, tiles in enumerate(ROW_GROUPS):
            h_codes.append(keep.tile([P, PASSES * len(tiles) * P], U32, align_bytes=64, name="h_codes%d" % m))
            h_scales.append(keep.tile([P, PASSES * len(tiles) * P], U8, align_bytes=64, name="h_scales%d" % m))
        w_codes = [keep.tile([P, PASSES * N_TILE], U32, align_bytes=64, name="w_codes%d" % n) for n in range(N_HALVES)]
        w_scales = [keep.tile([P, PASSES * N_TILE], U8, align_bytes=64, name="w_scales%d" % n) for n in range(N_HALVES)]
        stats_ps = {}
        part = [keep.tile([P, GROUPS_PER_PASS, 2], F32, name="part%d" % g) for g in range(PASSES)]
        parts_of = [[part[g]] for g in range(PASSES)]
        for g in range(PASSES):
            for i in range(1, len(PIECES[g])):
                more = keep.tile([P, GROUPS_PER_PASS, 2], F32, name="more%d_%d" % (g, i))
                nc.vector.memset(more[:], 0.0)
                parts_of[g].append(more)
        quad = [P, PACK]
        gain = [keep.tile(quad, F32, name="gain%d" % g) for g in range(PASSES)]
        shift = [keep.tile(quad, F32, name="shift%d" % g) for g in range(PASSES)]
        skip = keep.tile([P, 1], F32)
        moments = [keep.tile([P, 2], F32, name="moments%d" % g) for g in range(PASSES)]
        negvar = [keep.tile([P, 1], F32, name="negvar%d" % g) for g in range(PASSES)]
        eps = keep.tile([P, 1], F32)
        nc.vector.memset(eps[:], 0.0)
        nc.vector.tensor_scalar(out=eps[:], in0=eps[:], scalar1=EPS_GN, scalar2=None, op0=ALU.add)
        rstd = [keep.tile([P, 1], F32, name="rstd%d" % g) for g in range(PASSES)]
        nc.scalar.activation(out=rstd[0][:], in_=eps[:], func=ACT.Abs_reciprocal_sqrt)

        def spread_gn():
            bank = turned.tile([P, PASSES, PACK, 2], F32, tag="w3", name="gn_ps")
            for g in range(PASSES):
                for t in range(PACK):
                    channels = gn_rows[:, g * K_PASS + t : (g + 1) * K_PASS - PACK + t + 1 : PACK]
                    nc.tensor.matmul(out=bank[:, g, t, :], lhsT=channels, rhs=first_two[:], start=True, stop=True)
            return bank

        def new_stats(g):
            stats_ps[g] = turned.tile([P, 2 * SIDE + 4], F32, tag=STATS_BANKS[g % 2], name="stats_ps")

        def sums(g):
            for u in range(GROUPS_PER_PASS):
                if (g, u) in ON_TENSOR:
                    continue
                for j in range(ROW_TILES):
                    for c in range(2):
                        at = PAD + u * GROUP + c * P
                        nc.tensor.matmul(
                            out=stats_ps[g][:, u * (2 * SIDE - 3) : u * (2 * SIDE - 3) + 1],
                            lhsT=h_raw[g][:, j, at : at + P], rhs=ones[:],
                            start=(j == 0 and c == 0), stop=(j == ROW_TILES - 1 and c == 1),
                        )

        def keep_sums(g):
            nc.vector.tensor_copy(out=part[g][:, :, 0], in_=stats_ps[g][:, 0 : 2 * SIDE - 2 : 2 * SIDE - 3])

        def squares_on_scalar(g, u, i):
            rows = slice(sum(PIECES[g][:i]), sum(PIECES[g][: i + 1]))
            scratch = stage.tile([P, ROW_TILES, GROUP], BF16, name="scratch_s")
            nc.scalar.activation(
                out=scratch[:, 0 : PIECES[g][i], :], in_=h_raw[g][:, rows, PAD + u * GROUP : PAD + (u + 1) * GROUP],
                func=ACT.Square, accum_out=parts_of[g][i][:, u, 1:2],
            )

        def squares_on_vector(g, u, i):
            rows = slice(sum(PIECES[g][:i]), sum(PIECES[g][: i + 1]))
            group = h_raw[g][:, rows, PAD + u * GROUP : PAD + (u + 1) * GROUP]
            scratch = stage.tile([P, ROW_TILES, GROUP], BF16, name="scratch_v")
            nc.vector.scalar_tensor_tensor(
                out=scratch[:, 0 : PIECES[g][i], :], in0=group, scalar=1.0, in1=group, op0=ALU.mult, op1=ALU.mult,
                accum_out=parts_of[g][i][:, u, 1:2],
            )

        def products(g, u):
            flat = h_raw[g][:].rearrange("p j c -> p (j c)")
            for j in range(ROW_TILES):
                for e in range(2):
                    at = j * PITCH + PAD + u * GROUP + e
                    moving = at - 2 if u == 0 else at
                    nc.tensor.matmul(
                        out=stats_ps[g][:, u * (SIDE + 1) : u * (SIDE + 1) + P + 1],
                        lhsT=flat[:, at : at + GROUP - 1 : 2], rhs=flat[:, moving : moving + GROUP + 1 : 2],
                        start=(j == 0 and e == 0), stop=(j == ROW_TILES - 1 and e == 1),
                    )

        def diagonal(g, u):
            scratch = stage.tile([P, P], F32, name="scratch_d")
            nc.vector.scalar_tensor_tensor(
                out=scratch[:], in0=stats_ps[g][:, u * SIDE + 1 : u * SIDE + 1 + P], scalar=1.0, in1=ident_f32[:],
                op0=ALU.mult, op1=ALU.mult, accum_out=part[g][:, u, 1:2],
            )

        def squares(g, i):
            if (g, 1) not in ON_TENSOR:
                squares_on_vector(g, 1, i)
            squares_on_scalar(g, 0, i)

        def totals(g):
            for i, sums_of in enumerate(parts_of[g]):
                nc.tensor.matmul(
                    out=stats_ps[g][:, 2 * SIDE : 2 * SIDE + 4], lhsT=minus_mean_of[:],
                    rhs=sums_of[:].rearrange("p u k -> p (u k)"),
                    start=(i == 0), stop=(i == len(parts_of[g]) - 1),
                )

        def square_of_mean(g):
            half = P // GROUPS_PER_PASS
            for u in range(GROUPS_PER_PASS):
                channels = slice(u * half, (u + 1) * half)
                at = 2 * SIDE + 2 * u
                nc.vector.tensor_copy(out=moments[g][channels, :], in_=stats_ps[g][channels, at : at + 2])
            nc.vector.scalar_tensor_tensor(
                out=negvar[g][:], in0=moments[g][:, 0:1], scalar=moments[g][:, 0:1], in1=moments[g][:, 1:2],
                op0=ALU.mult, op1=ALU.add,
            )

        def gain_of(g):
            nc.scalar.activation(
                out=rstd[g][:], in_=negvar[g][:], func=ACT.Abs_reciprocal_sqrt, scale=-1.0, bias=eps[:]
            )
            nc.scalar.activation(out=gain[g][:], in_=gn_sb[:, g, :, 0], func=ACT.Identity, scale=rstd[g][:, 0:1])

        def shift_of(g):
            nc.vector.scalar_tensor_tensor(
                out=shift[g][:], in0=gain[g][:], scalar=moments[g][:, 0:1], in1=gn_sb[:, g, :, 1],
                op0=ALU.mult, op1=ALU.add,
            )

        def transpose_h(m, g):
            words = h_raw[g][:].rearrange("p j c -> p (j c)").bitcast(F32).rearrange("p (j w) -> p j w", j=ROW_TILES + 1)
            tiles = ROW_GROUPS[m]
            tag = H_BANKS[1 + g % 2] if m == 0 else (H_BANKS[g] if m == 1 else LATE_BANKS[g])
            bank = turned.tile([P, 2, len(tiles), P], F32, tag=tag, name="hT")
            for u in range(2):
                for i, j in enumerate(tiles):
                    nc.tensor.transpose(out=bank[:, u, i, :], in_=words[:, j, PAD // 2 + u : PITCH // 2 : 2], identity=ident_f32[:])
            return bank

        def normalise_all(m, g, bank):
            rows = len(ROW_GROUPS[m]) * P
            planes = planes_pool.tile([P, PACK, rows], BF16, name="planes")
            for t in range(PACK):
                u, e = t // 2, t % 2
                values = bank[:, u].rearrange("p i r -> p (i r)").bitcast(BF16).rearrange("p (r e) -> p e r", e=2)[:, e, :]
                nc.scalar.activation(
                    out=planes[:, t, :], in_=values, func=ACT.Identity,
                    scale=gain[g][:, t : t + 1], bias=shift[g][:, t : t + 1],
                )
            return planes

        def regroup(g, planes, grouped, on_scalar):
            copy = nc.scalar.copy if on_scalar else nc.vector.tensor_copy
            copy(
                out=grouped[:, g].rearrange("p (c i) t -> p c t i", i=8),
                in_=planes[:].rearrange("p t (c i) -> p c t i", i=8),
            )

        def new_grouped(m):
            return stage.tile([P, PASSES, len(ROW_GROUPS[m]) * P, PACK], BF16, align_bytes=64, name="h_grouped")

        def quantise_h(m, g0, g1, grouped):
            rows = len(ROW_GROUPS[m]) * P
            cols = slice(g0 * rows, g1 * rows)
            nc.vector.quantize_mx(
                out=h_codes[m][:, cols].bitcast(FP8X4), scales=h_scales[m][:, cols],
                in_=grouped[:, g0:g1].rearrange("p g s t -> p (g s t)"),
            )

        def transpose_w(c, a):
            bank = turned.tile([P, 2, 2, P], F32, tag=W_BANKS[a], name="wT")
            for i in range(2):
                channels = w_raw[c][:, 2 * (a % 2) + i, a // 2 * K_PASS : (a // 2 + 1) * K_PASS]
                words = channels.bitcast(F32).rearrange("p (q u) -> p u q", u=2)
                for u in range(2):
                    nc.tensor.transpose(out=bank[:, i, u, :], in_=words[:, u, :], identity=ident_f32[:])
            return bank

        def copy_w(grouped, bank, a, on_scalar):
            grouped_words = grouped[:].bitcast(F32).rearrange("p (a i m u) -> p a i m u", a=4, i=2, u=2)
            copy = nc.scalar.copy if on_scalar else nc.vector.tensor_copy
            copy(out=grouped_words[:, a], in_=bank[:].rearrange("p i u m -> p i m u"))

        def quantise_w(c, grouped):
            n, words = c % 2, slice(c // 2 * 2 * N_TILE, (c // 2 + 1) * 2 * N_TILE)
            nc.vector.quantize_mx(out=w_codes[n][:, words].bitcast(FP8X4), scales=w_scales[n][:, words], in_=grouped[:])

        def multiply(acc, m, i, n, c0, width, g):
            first = (g * len(ROW_GROUPS[m]) + i) * P
            rows = slice(first, first + P)
            words = slice(g * N_TILE + c0, g * N_TILE + c0 + width)
            nc.tensor.matmul_mx(
                out=acc[:], lhsT=h_codes[m][:, rows].bitcast(FP8X4), lhsT_scale=h_scales[m][:, rows],
                rhs=w_codes[n][:, words].bitcast(FP8X4), rhs_scale=w_scales[n][:, words],
                start=(g == 0), stop=(g == PASSES - 1),
            )

        def multiply_tile(m, i, n, c0, width, waiting):
            acc = new_acc(width)
            cols = slice(n * N_TILE + c0, n * N_TILE + c0 + width)
            for g in range(PASSES):
                multiply(acc, m, i, n, c0, width, g)
            waiting.append((acc, ROW_GROUPS[m][i], cols, width))

        def finish(waiting):
            acc, j, cols, width = waiting[0]
            waiting.remove(waiting[0])
            result = results.tile([P, width], F32, name="result")
            nc.vector.scalar_tensor_tensor(
                out=result[:], in0=x_sb[:, j, cols], scalar=skip[:, 0:1], in1=acc[:], op0=ALU.mult, op1=ALU.add
            )
            nc.sync.dma_start(out=out_rows[:, j, cols], in_=result[:])

        acc_tags = []

        def new_w_grouped():
            return stage.tile([P, DM * PACK], BF16, align_bytes=64, name="w_grouped")

        def move_w(g, a):
            copy_w(wg[g], transpose_w(g, a), a, W_ORDER.index(a) % 2 == 1)

        def new_acc(width):
            tag = ACC_TAGS[len(acc_tags) % len(ACC_TAGS)]
            acc_tags.append(tag)
            return turned.tile([P, width], F32, tag=tag, name="acc")

        hb = {}
        pl = {}
        wg = {}
        hb1 = {}
        pl1 = {}
        grouped = {0: new_grouped(0), 1: new_grouped(1)}
        for k in range(PASSES + 2):
            now, last, older = k < PASSES, 0 <= k - 1 < PASSES, 0 <= k - 2 < PASSES
            if now:
                new_stats(k)
                if (k, 1) in ON_TENSOR:
                    products(k, 1)
            if older:
                quantise_w(k - 2, wg[k - 2])
            if now:
                for i in range(len(PIECES[k])):
                    if not (k == 1 and i == 0):
                        squares(k, i)
                sums(k)
                if (k, 1) in ON_TENSOR:
                    diagonal(k, 1)
            if last:
                pl[k - 1] = normalise_all(0, k - 1, hb[k - 1])
            if now:
                keep_sums(k)
                hb[k] = transpose_h(0, k)
            if k == 0:
                gn_bank = spread_gn()
            if last:
                wg[k - 1] = new_w_grouped()
                move_w(k - 1, W_ORDER[0])
                move_w(k - 1, W_ORDER[1])
            if now:
                totals(k)
                if k == 0:
                    squares(1, 0)
                square_of_mean(k)
            if k == 0:
                nc.vector.tensor_copy(out=gn_sb[:], in_=gn_bank[:])
            if last:
                regroup(k - 1, pl[k - 1], grouped[0], False)
                move_w(k - 1, W_ORDER[2])
            if now:
                gain_of(k)
            if last:
                move_w(k - 1, W_ORDER[3])
            if k == PASSES - 1:
                hb1[0] = transpose_h(1, 0)
            if now:
                shift_of(k)
            if k == PASSES:
                for g in range(PASSES):
                    if g > 0:
                        hb1[g] = transpose_h(1, g)
                    pl1[g] = normalise_all(1, g, hb1[g])
            if last and k % 2 == 0:
                quantise_h(0, k - 2, k, grouped[0])
        nc.vector.tensor_copy(out=skip[:], in_=skip_bf[:])

        waiting = []
        groups = len(ROW_GROUPS)
        for m in range(1, groups + 1):
            if 1 < m < groups:
                grouped[m] = new_grouped(m)
            tiles = [(m - 1, i, n) for n in range(N_HALVES) for i in range(len(ROW_GROUPS[m - 1]))]
            for s in range(PASSES):
                run = RUNS[m]
                if m + 1 < groups and s % run == 0:
                    for g in range(s, s + run):
                        hb1[g] = transpose_h(m + 1, g)
                if m < groups:
                    regroup(s, pl1[s], grouped[m], (m, s) in S_RG)
                    if s == PASSES - 1:
                        quantise_h(m, 0, PASSES, grouped[m])
                if len(waiting) > (1 if m < groups else 0):
                    finish(waiting)
                if m + 1 < groups:
                    pl1[s] = normalise_all(m + 1, s, hb1[s])
                if len(tiles) == PASSES:
                    mine = tiles[s : s + 1]
                else:
                    mine = tiles[s // 2 : s // 2 + 1] if s % 2 == 1 else []
                for m1, i, n in mine:
                    if m == groups and s == PASSES - 1:
                        multiply_tile(m1, i, n, 0, N_TILE // 2, waiting)
                        finish(waiting)
                        multiply_tile(m1, i, n, N_TILE // 2, N_TILE // 4, waiting)
                        finish(waiting)
                        multiply_tile(m1, i, n, 3 * N_TILE // 4, N_TILE // 4, waiting)
                    else:
                        multiply_tile(m1, i, n, 0, N_TILE, waiting)
        for i in range(len(waiting)):
            finish(waiting)
